import numpy as np
import ml_dtypes


def mxq(x, axis, fmt="e4m3"):
    dtype, down = {"e4m3": (ml_dtypes.float8_e4m3fn, 7), "e5m2": (ml_dtypes.float8_e5m2, 14)}[fmt]
    v = np.moveaxis(np.asarray(x, np.float32).astype(ml_dtypes.bfloat16).astype(np.float64), axis, -1)
    blocks = v.reshape(v.shape[:-1] + (-1, 32))
    amax = np.abs(blocks).max(-1, keepdims=True)
    byte = np.maximum(np.where(amax > 0, np.frexp(amax)[1] - 1 + 127, 0) - down, 1)
    scale = np.exp2(byte - 127.0)
    codes = (blocks / scale).astype(np.float32).astype(dtype).astype(np.float64)
    return np.moveaxis((codes * scale).reshape(v.shape), -1, axis)


WIDE = False


def mx_kscale(k):
    if not WIDE:
        return np.ones(k)
    levels = np.array([10, -10, 5, -5, 0])
    a = np.random.permutation(np.resize(levels, k // 512 * 4)).reshape(k // 512, 4)
    idx = np.arange(k)
    return np.exp2(a[idx // 512, idx % 128 // 32])


BF16 = ml_dtypes.bfloat16


def bf(x):
    return np.asarray(x, np.float32).astype(BF16)


def f64(x):
    return np.asarray(x).astype(np.float64)


E2M1 = np.array([0.0, 0.5, 1.0, 1.5, 2.0, 3.0, 4.0, 6.0, -0.0, -0.5, -1.0, -1.5, -2.0, -3.0, -4.0, -6.0])


def pack_weight(w, fmt):
    k, n = w.shape
    w = f64(bf(w)).reshape(k // 32, 32, n)
    amax = np.abs(w).max(1)
    if fmt == "e4m3":
        byte = np.frexp(amax)[1] - 1 + 127 - 7
    else:
        mant, ex = np.frexp(amax / 6.0)
        byte = np.where(mant > 0.5, ex, ex - 1) + 127
    byte = np.clip(np.where(amax > 0, byte, 1), 1, 254)
    scaled = (w * np.exp2(127.0 - byte)[:, None, :]).reshape(k, n).astype(np.float32)
    by_word = np.ascontiguousarray(scaled.reshape(k // 512, 128, 4, n).transpose(0, 1, 3, 2))
    if fmt == "e4m3":
        words = by_word.astype(ml_dtypes.float8_e4m3fn).view(np.uint8)
    else:
        c = by_word.astype(ml_dtypes.float4_e2m1fn).view(np.uint8) & 0xF
        words = c[..., 0::2] | (c[..., 1::2] << 4)
    return np.ascontiguousarray(words), np.ascontiguousarray(byte.astype(np.uint8).reshape(k // 512, 16, n))


def unpack_weight(words, scales, fmt):
    g, p, n, _ = words.shape
    if fmt == "e4m3":
        vals = np.ascontiguousarray(words).view(ml_dtypes.float8_e4m3fn).astype(np.float64)
    else:
        nib = np.empty((g, p, n, 4), np.uint8)
        nib[..., 0::2] = words & 0xF
        nib[..., 1::2] = words >> 4
        vals = E2M1[nib]
    vals = vals * np.repeat(np.exp2(scales.astype(np.float64) - 127.0), 8, axis=1)[..., None]
    return vals.transpose(0, 1, 3, 2).reshape(g * 512, n)


B, IN, OUT = 512, 1024, 1024
G = 3 * OUT
FMT = "e4m3"


def sigmoid(v):
    return 1.0 / (1.0 + np.exp(-v))


def setup_inputs():
    s = mx_kscale(OUT)
    xg = bf(np.random.standard_normal((B, G)) * 0.75)
    hx = bf(np.random.standard_normal((B, OUT)) * s)
    cx = bf(np.random.standard_normal((B, OUT)))
    td0 = bf(np.random.uniform(0.0, 1.0, B))
    td1 = bf(np.random.uniform(0.0, 1.0, B))
    w_hh = np.random.standard_normal((G, OUT)) * 0.7 / np.sqrt(OUT) / s
    w_pi = np.random.standard_normal((OUT, OUT)) * 0.7 / np.sqrt(OUT)
    w_pf = np.random.standard_normal((OUT, OUT)) * 0.7 / np.sqrt(OUT)
    b_hh = bf(np.random.standard_normal(G) * 0.3)
    a = bf(1.0 + 0.1 * np.random.standard_normal(1))
    b = bf(0.5 + 0.1 * np.random.standard_normal(1))
    w_hh_words, w_hh_scales = pack_weight(np.ascontiguousarray(w_hh.T), FMT)
    w_pi_words, w_pi_scales = pack_weight(np.ascontiguousarray(w_pi.T), FMT)
    w_pf_words, w_pf_scales = pack_weight(np.ascontiguousarray(w_pf.T), FMT)
    return {
        "xg": xg,
        "hx": hx,
        "cx": cx,
        "td0": td0,
        "td1": td1,
        "w_hh_words": w_hh_words,
        "w_hh_scales": w_hh_scales,
        "w_pi_words": w_pi_words,
        "w_pi_scales": w_pi_scales,
        "w_pf_words": w_pf_words,
        "w_pf_scales": w_pf_scales,
        "b_hh": b_hh,
        "a": a,
        "b": b,
    }


def reference(xg, hx, cx, td0, td1, w_hh_words, w_hh_scales, w_pi_words, w_pi_scales, w_pf_words, w_pf_scales, b_hh, a, b):
    c = f64(cx)
    cq = mxq(c, 1, "e4m3")
    gates = f64(xg) + (mxq(f64(hx), 1, "e4m3") @ unpack_weight(w_hh_words, w_hh_scales, FMT)) + f64(b_hh)
    i_g, f_g, g_g = np.split(gates, 3, axis=1)
    i_g = sigmoid(i_g + (cq @ unpack_weight(w_pi_words, w_pi_scales, FMT)))
    f_g = sigmoid(f_g + (cq @ unpack_weight(w_pf_words, w_pf_scales, FMT)))
    g_g = np.tanh(g_g)
    forcoff = (f64(a) * np.exp(-f64(b) * f64(td0)))[:, None]
    incoff = (f64(a) * np.exp(-f64(b) * f64(td1)))[:, None]
    f_g = forcoff * f_g
    i_g = incoff * i_g
    return f_g * c + i_g * g_g

@@ -1,0 +1,234 @@
+from contextlib import ExitStack
+
+import concourse.mybir as mybir
+from concourse.masks import make_identity
+
+F32 = mybir.dt.float32
+BF16 = mybir.dt.bfloat16
+I32 = mybir.dt.int32
+U32 = mybir.dt.uint32
+U8 = mybir.dt.uint8
+FP8X4 = mybir.dt.float8_e4m3fn_x4
+ADD = mybir.AluOpType.add
+MULT = mybir.AluOpType.mult
+FUNC = mybir.ActivationFunctionType
+
+P = 128
+BATCH = 512
+HID = 1024
+M_TILES = BATCH // P
+K_PASS = 512
+K_GROUPS = HID // K_PASS
+N_TILE = 512
+HALVES = HID // N_TILE
+GATE_COLUMN = {"i": 0, "f": HID, "g": 2 * HID}
+VECTOR_M_TILES = 2
+
+FLOPS = 2 * BATCH * HID * 5 * HID
+
+
+def load_weight_words(nc, words_tile, words, first_column):
+    by_partition = words.rearrange("kg p n t -> p kg (n t)")
+    columns = by_partition[:, :, 4 * first_column : 4 * (first_column + N_TILE)]
+    nc.sync.dma_start(out=words_tile[:].bitcast(I32), in_=columns.bitcast(I32))
+
+
+def quantise_batch_tile(nc, psum_t, ident_f32, x_rows, grouped, codes, scales):
+    words = x_rows.bitcast(F32)
+    xt = psum_t.tile([P, K_GROUPS * 2, P], F32, name="xt")
+    for kg in range(K_GROUPS):
+        for u in range(2):
+            nc.tensor.transpose(
+                xt[:, 2 * kg + u, :],
+                words[:, 256 * kg + u : 256 * (kg + 1) : 2],
+                ident_f32[:],
+            )
+    nc.scalar.copy(
+        out=grouped.bitcast(F32).rearrange("p (kg r u) -> p kg r u", kg=K_GROUPS, u=2),
+        in_=xt[:].rearrange("p (kg u) r -> p kg r u", u=2),
+    )
+    nc.vector.quantize_mx(out=codes.bitcast(FP8X4), scales=scales, in_=grouped)
+
+
+def tile_ircnn_lstmcell_pa_kernel(
+    tc, xg, hx, cx, td0, td1,
+    w_hh_words, w_hh_scales, w_pi_words, w_pi_scales, w_pf_words, w_pf_scales,
+    b_hh, a, b, out,
+):
+    nc = tc.nc
+    with ExitStack() as ctx:
+        keep = ctx.enter_context(tc.tile_pool(name="keep", bufs=1))
+        results = ctx.enter_context(tc.tile_pool(name="results", bufs=4))
+        psum_t = ctx.enter_context(tc.psum_pool(name="psum_t", bufs=2))
+        psum_acc = ctx.enter_context(tc.psum_pool(name="psum_acc", bufs=4))
+        psum_misc = ctx.enter_context(tc.psum_pool(name="psum_misc", bufs=2))
+
+        ident_f32 = keep.tile([P, P], F32, name="ident_f32")
+        make_identity(nc, ident_f32[:])
+        ident_bf16 = keep.tile([P, P], BF16, name="ident_bf16")
+        make_identity(nc, ident_bf16[:])
+
+        planes = keep.tile([P, 3 * HID], U8, name="planes", align_bytes=64)
+        nc.vector.memset(planes[:].bitcast(I32), 0)
+        bias_rows = keep.tile([P, N_TILE], BF16, name="bias_rows")
+        nc.vector.memset(bias_rows[:].bitcast(I32), 0)
+        td_rows = keep.tile([P, P], BF16, name="td_rows")
+        nc.vector.memset(td_rows[:].bitcast(I32), 0)
+
+        nc.sync.dma_start(out=bias_rows[0:6, :], in_=b_hh.rearrange("(j n) -> j n", n=N_TILE))
+        for quad in range(4):
+            nc.sync.dma_start(
+                out=planes[32 * quad : 32 * quad + 8, :].bitcast(I32),
+                in_=w_hh_scales[:, 4 * quad : 4 * quad + 4, :].bitcast(I32),
+            )
+        for scales_in, first_column in ((w_pi_scales, 0), (w_pf_scales, HID)):
+            for quad in range(4):
+                nc.sync.dma_start(
+                    out=planes[32 * quad + 8 : 32 * quad + 16, first_column : first_column + HID].bitcast(I32),
+                    in_=scales_in[:, 4 * quad : 4 * quad + 4, :].bitcast(I32),
+                )
+
+        hx_sb = keep.tile([P, M_TILES, HID], BF16, name="hx_sb")
+        cx_sb = keep.tile([P, M_TILES, HID], BF16, name="cx_sb")
+        xg_sb = {}
+        hh_words = {}
+        peep_words = {}
+        xg_by_tile = xg.rearrange("(m p) n -> p m n", p=P)
+
+        def load_activations(x_sb, x):
+            by_tile = x.rearrange("(m p) k -> p m k", p=P)
+            for first in range(0, M_TILES, 2):
+                nc.sync.dma_start(out=x_sb[:, first : first + 2, :], in_=by_tile[:, first : first + 2, :])
+
+        def load_gate(gate, half):
+            column = GATE_COLUMN[gate] + half * N_TILE
+            xg_sb[gate, half] = keep.tile([P, M_TILES, N_TILE], BF16, name="xg_%s%d" % (gate, half))
+            nc.sync.dma_start(out=xg_sb[gate, half][:], in_=xg_by_tile[:, :, column : column + N_TILE])
+            hh_words[gate, half] = keep.tile(
+                [P, K_GROUPS, N_TILE], U32, name="hh_%s%d" % (gate, half), align_bytes=64
+            )
+            load_weight_words(nc, hh_words[gate, half], w_hh_words, column)
+            if gate != "g":
+                peep_words[gate, half] = keep.tile(
+                    [P, K_GROUPS, N_TILE], U32, name="peep_%s%d" % (gate, half), align_bytes=64
+                )
+                load_weight_words(
+                    nc, peep_words[gate, half], w_pi_words if gate == "i" else w_pf_words, half * N_TILE
+                )
+
+        load_activations(hx_sb, hx)
+        load_gate("g", 0)
+        load_activations(cx_sb, cx)
+        load_gate("i", 0)
+        load_gate("f", 0)
+        for gate in ("g", "i", "f"):
+            load_gate(gate, 1)
+
+        nc.gpsimd.dma_start(out=td_rows[0:M_TILES, :], in_=td0.rearrange("(m p) -> m p", p=P))
+        nc.gpsimd.dma_start(out=td_rows[M_TILES : 2 * M_TILES, :], in_=td1.rearrange("(m p) -> m p", p=P))
+        a_bf16 = keep.tile([P, 1], BF16, name="a_bf16")
+        nc.gpsimd.dma_start(out=a_bf16[:], in_=a.partition_broadcast(P))
+        b_bf16 = keep.tile([P, 1], BF16, name="b_bf16")
+        nc.gpsimd.dma_start(out=b_bf16[:], in_=b.partition_broadcast(P))
+
+        bias_all = keep.tile([P, 6, N_TILE], BF16, name="bias_all")
+        for j in range(6):
+            bias_ps = psum_misc.tile([P, N_TILE], F32, name="bias_ps", tag="misc")
+            nc.tensor.matmul(
+                out=bias_ps[:],
+                lhsT=ident_bf16[:, j : j + 1].to_broadcast([P, P]),
+                rhs=bias_rows[:],
+                start=True,
+                stop=True,
+            )
+            nc.scalar.copy(out=bias_all[:, j, :], in_=bias_ps[:])
+
+        td_ps = psum_misc.tile([P, P], BF16, name="td_ps", tag="misc")
+        nc.tensor.transpose(td_ps[:], td_rows[:], ident_bf16[:])
+        minus_b = keep.tile([P, 1], F32, name="minus_b")
+        nc.vector.tensor_scalar_mul(out=minus_b[:], in0=b_bf16[:], scalar1=-1.0)
+        a_f32 = keep.tile([P, 1], F32, name="a_f32")
+        nc.vector.tensor_copy(out=a_f32[:], in_=a_bf16[:])
+        decay = keep.tile([P, 2 * M_TILES], F32, name="decay")
+        nc.scalar.activation(out=decay[:], in_=td_ps[:, 0 : 2 * M_TILES], func=FUNC.Exp, scale=minus_b[:, 0:1])
+        nc.vector.tensor_scalar_mul(out=decay[:], in0=decay[:], scalar1=a_f32[:, 0:1])
+
+        quantised = {}
+
+        def quantise(key, x_sb):
+            grouped = keep.tile([P, M_TILES, HID], BF16, name="grouped_" + key, align_bytes=64)
+            codes = keep.tile([P, M_TILES, K_GROUPS * P], U32, name="codes_" + key, align_bytes=64)
+            scales = keep.tile([P, M_TILES, K_GROUPS * P], U8, name="scales_" + key, align_bytes=64)
+            for m in range(M_TILES):
+                quantise_batch_tile(
+                    nc, psum_t, ident_f32, x_sb[:, m, :], grouped[:, m, :], codes[:, m, :], scales[:, m, :]
+                )
+            quantised[key] = (codes, scales)
+
+        gate_values = {}
+
+        def compute_gate(name, half):
+            column = GATE_COLUMN[name] + half * N_TILE
+            z = keep.tile([P, M_TILES, N_TILE], F32, name="z_%s%d" % (name, half))
+            gate_values[name, half] = z
+            bias = bias_all[:, column // N_TILE, :].unsqueeze(1)
+            split = VECTOR_M_TILES
+            nc.vector.tensor_tensor(
+                out=z[:, 0:split, :], in0=xg_sb[name, half][:, 0:split, :],
+                in1=bias.to_broadcast([P, split, N_TILE]), op=ADD,
+            )
+            nc.gpsimd.tensor_tensor(
+                out=z[:, split:M_TILES, :], in0=xg_sb[name, half][:, split:M_TILES, :],
+                in1=bias.to_broadcast([P, M_TILES - split, N_TILE]), op=ADD,
+            )
+            products = [("hx", hh_words[name, half], 0, column)]
+            if name != "g":
+                products.append(("cx", peep_words[name, half], 8, (0 if name == "i" else HID) + half * N_TILE))
+            last = len(products) * K_GROUPS - 1
+            for m in range(M_TILES):
+                acc = psum_acc.tile([P, N_TILE], F32, name="acc")
+                count = 0
+                for key, words, first, plane_column in products:
+                    codes, scales = quantised[key]
+                    for kg in range(K_GROUPS):
+                        nc.tensor.matmul_mx(
+                            out=acc[:],
+                            lhsT=codes[:, m, kg * P : (kg + 1) * P].bitcast(FP8X4),
+                            lhsT_scale=scales[:, m, kg * P : (kg + 1) * P],
+                            rhs=words[:, kg, :].bitcast(FP8X4),
+                            rhs_scale=planes[first + 4 * kg : P, plane_column : plane_column + N_TILE],
+                            start=(count == 0),
+                            stop=(count == last),
+                        )
+                        count += 1
+                nc.vector.tensor_tensor(out=z[:, m, :], in0=acc[:], in1=z[:, m, :], op=ADD)
+                nc.scalar.activation(
+                    out=z[:, m, :], in_=z[:, m, :], func=FUNC.Tanh if name == "g" else FUNC.Sigmoid
+                )
+
+        def combine(half):
+            columns = slice(half * N_TILE, (half + 1) * N_TILE)
+            for m in range(M_TILES):
+                i_g = gate_values["i", half][:, m, :]
+                f_g = gate_values["f", half][:, m, :]
+                g_g = gate_values["g", half][:, m, :]
+                nc.vector.scalar_tensor_tensor(
+                    out=i_g, in0=i_g, scalar=decay[:, M_TILES + m : M_TILES + m + 1], in1=g_g, op0=MULT, op1=MULT
+                )
+                nc.vector.scalar_tensor_tensor(
+                    out=f_g, in0=f_g, scalar=decay[:, m : m + 1], in1=cx_sb[:, m, columns], op0=MULT, op1=MULT
+                )
+                result = results.tile([P, N_TILE], F32, name="result")
+                nc.vector.tensor_tensor(out=result[:], in0=i_g, in1=f_g, op=ADD)
+                nc.sync.dma_start(out=out[m * P : (m + 1) * P, columns], in_=result[:])
+
+        quantise("hx", hx_sb)
+        compute_gate("g", 0)
+        quantise("cx", cx_sb)
+        compute_gate("i", 0)
+        compute_gate("f", 0)
+        combine(0)
+        compute_gate("g", 1)
+        compute_gate("i", 1)
+        compute_gate("f", 1)
+        combine(1)

@@ -22,7 +22,8 @@ K_GROUPS = HID // K_PASS
 N_TILE = 512
 HALVES = HID // N_TILE
 GATE_COLUMN = {"i": 0, "f": HID, "g": 2 * HID}
-VECTOR_M_TILES = 2
+BLOCKS = (("g", 0), ("g", 1), ("i", 0), ("f", 0), ("i", 1), ("f", 1))
+TENSOR_M_TILES = 2
 
 FLOPS = 2 * BATCH * HID * 5 * HID
 
@@ -31,23 +32,6 @@ def load_weight_words(nc, words_tile, words, first_column):
     by_partition = words.rearrange("kg p n t -> p kg (n t)")
     columns = by_partition[:, :, 4 * first_column : 4 * (first_column + N_TILE)]
     nc.sync.dma_start(out=words_tile[:].bitcast(I32), in_=columns.bitcast(I32))
-
-
-def quantise_batch_tile(nc, psum_t, ident_f32, x_rows, grouped, codes, scales):
-    words = x_rows.bitcast(F32)
-    xt = psum_t.tile([P, K_GROUPS * 2, P], F32, name="xt")
-    for kg in range(K_GROUPS):
-        for u in range(2):
-            nc.tensor.transpose(
-                xt[:, 2 * kg + u, :],
-                words[:, 256 * kg + u : 256 * (kg + 1) : 2],
-                ident_f32[:],
-            )
-    nc.scalar.copy(
-        out=grouped.bitcast(F32).rearrange("p (kg r u) -> p kg r u", kg=K_GROUPS, u=2),
-        in_=xt[:].rearrange("p (kg u) r -> p kg r u", u=2),
-    )
-    nc.vector.quantize_mx(out=codes.bitcast(FP8X4), scales=scales, in_=grouped)
 
 
 def tile_ircnn_lstmcell_pa_kernel(
@@ -59,9 +43,8 @@ def tile_ircnn_lstmcell_pa_kernel(
     with ExitStack() as ctx:
         keep = ctx.enter_context(tc.tile_pool(name="keep", bufs=1))
         results = ctx.enter_context(tc.tile_pool(name="results", bufs=4))
-        psum_t = ctx.enter_context(tc.psum_pool(name="psum_t", bufs=2))
-        psum_acc = ctx.enter_context(tc.psum_pool(name="psum_acc", bufs=4))
-        psum_misc = ctx.enter_context(tc.psum_pool(name="psum_misc", bufs=2))
+        banks = ctx.enter_context(tc.psum_pool(name="banks", bufs=8))
+        ctx.enter_context(tc.manual_schedule())
 
         ident_f32 = keep.tile([P, P], F32, name="ident_f32")
         make_identity(nc, ident_f32[:])
@@ -75,19 +58,6 @@ def tile_ircnn_lstmcell_pa_kernel(
         td_rows = keep.tile([P, P], BF16, name="td_rows")
         nc.vector.memset(td_rows[:].bitcast(I32), 0)
 
-        nc.sync.dma_start(out=bias_rows[0:6, :], in_=b_hh.rearrange("(j n) -> j n", n=N_TILE))
-        for quad in range(4):
-            nc.sync.dma_start(
-                out=planes[32 * quad : 32 * quad + 8, :].bitcast(I32),
-                in_=w_hh_scales[:, 4 * quad : 4 * quad + 4, :].bitcast(I32),
-            )
-        for scales_in, first_column in ((w_pi_scales, 0), (w_pf_scales, HID)):
-            for quad in range(4):
-                nc.sync.dma_start(
-                    out=planes[32 * quad + 8 : 32 * quad + 16, first_column : first_column + HID].bitcast(I32),
-                    in_=scales_in[:, 4 * quad : 4 * quad + 4, :].bitcast(I32),
-                )
-
         hx_sb = keep.tile([P, M_TILES, HID], BF16, name="hx_sb")
         cx_sb = keep.tile([P, M_TILES, HID], BF16, name="cx_sb")
         xg_sb = {}
@@ -97,17 +67,27 @@ def tile_ircnn_lstmcell_pa_kernel(
 
         def load_activations(x_sb, x):
             by_tile = x.rearrange("(m p) k -> p m k", p=P)
-            for first in range(0, M_TILES, 2):
-                nc.sync.dma_start(out=x_sb[:, first : first + 2, :], in_=by_tile[:, first : first + 2, :])
+            for m in range(0, M_TILES, 2):
+                nc.sync.dma_start(out=x_sb[:, m : m + 2, :], in_=by_tile[:, m : m + 2, :])
 
-        def load_gate(gate, half):
+        def load_scales(scales_in, first_partition, first_column, width):
+            for quad in range(4):
+                start = 32 * quad + first_partition
+                nc.sync.dma_start(
+                    out=planes[start : start + 8, first_column : first_column + width].bitcast(I32),
+                    in_=scales_in[:, 4 * quad : 4 * quad + 4, :].bitcast(I32),
+                )
+
+        def load_xg(gate, half):
             column = GATE_COLUMN[gate] + half * N_TILE
             xg_sb[gate, half] = keep.tile([P, M_TILES, N_TILE], BF16, name="xg_%s%d" % (gate, half))
             nc.sync.dma_start(out=xg_sb[gate, half][:], in_=xg_by_tile[:, :, column : column + N_TILE])
+
+        def load_weights(gate, half):
             hh_words[gate, half] = keep.tile(
                 [P, K_GROUPS, N_TILE], U32, name="hh_%s%d" % (gate, half), align_bytes=64
             )
-            load_weight_words(nc, hh_words[gate, half], w_hh_words, column)
+            load_weight_words(nc, hh_words[gate, half], w_hh_words, GATE_COLUMN[gate] + half * N_TILE)
             if gate != "g":
                 peep_words[gate, half] = keep.tile(
                     [P, K_GROUPS, N_TILE], U32, name="peep_%s%d" % (gate, half), align_bytes=64
@@ -116,13 +96,19 @@ def tile_ircnn_lstmcell_pa_kernel(
                     nc, peep_words[gate, half], w_pi_words if gate == "i" else w_pf_words, half * N_TILE
                 )
 
+        nc.sync.dma_start(out=bias_rows[0:6, :], in_=b_hh.rearrange("(j n) -> j n", n=N_TILE))
         load_activations(hx_sb, hx)
-        load_gate("g", 0)
-        load_activations(cx_sb, cx)
-        load_gate("i", 0)
-        load_gate("f", 0)
-        for gate in ("g", "i", "f"):
-            load_gate(gate, 1)
+        load_xg(*BLOCKS[0])
+        load_scales(w_hh_scales, 0, 0, 3 * HID)
+        load_xg(*BLOCKS[1])
+        for step, block in enumerate(BLOCKS):
+            if step == 2:
+                load_scales(w_pi_scales, 8, 0, HID)
+                load_scales(w_pf_scales, 8, HID, HID)
+                load_activations(cx_sb, cx)
+            load_weights(*block)
+            if step + 2 < len(BLOCKS):
+                load_xg(*BLOCKS[step + 2])
 
         nc.gpsimd.dma_start(out=td_rows[0:M_TILES, :], in_=td0.rearrange("(m p) -> m p", p=P))
         nc.gpsimd.dma_start(out=td_rows[M_TILES : 2 * M_TILES, :], in_=td1.rearrange("(m p) -> m p", p=P))
@@ -132,26 +118,31 @@ def tile_ircnn_lstmcell_pa_kernel(
         nc.gpsimd.dma_start(out=b_bf16[:], in_=b.partition_broadcast(P))
 
         bias_all = keep.tile([P, 6, N_TILE], BF16, name="bias_all")
-        for j in range(6):
-            bias_ps = psum_misc.tile([P, N_TILE], F32, name="bias_ps", tag="misc")
-            nc.tensor.matmul(
-                out=bias_ps[:],
-                lhsT=ident_bf16[:, j : j + 1].to_broadcast([P, P]),
-                rhs=bias_rows[:],
-                start=True,
-                stop=True,
-            )
-            nc.scalar.copy(out=bias_all[:, j, :], in_=bias_ps[:])
+        gate_values = {}
 
-        td_ps = psum_misc.tile([P, P], BF16, name="td_ps", tag="misc")
-        nc.tensor.transpose(td_ps[:], td_rows[:], ident_bf16[:])
-        minus_b = keep.tile([P, 1], F32, name="minus_b")
-        nc.vector.tensor_scalar_mul(out=minus_b[:], in0=b_bf16[:], scalar1=-1.0)
-        a_f32 = keep.tile([P, 1], F32, name="a_f32")
-        nc.vector.tensor_copy(out=a_f32[:], in_=a_bf16[:])
-        decay = keep.tile([P, 2 * M_TILES], F32, name="decay")
-        nc.scalar.activation(out=decay[:], in_=td_ps[:, 0 : 2 * M_TILES], func=FUNC.Exp, scale=minus_b[:, 0:1])
-        nc.vector.tensor_scalar_mul(out=decay[:], in0=decay[:], scalar1=a_f32[:, 0:1])
+        def bias_selector(gate, half):
+            j = (GATE_COLUMN[gate] + half * N_TILE) // N_TILE
+            return ident_bf16[:, j : j + 1].to_broadcast([P, P])
+
+        def spread_bias(gate, half):
+            j = (GATE_COLUMN[gate] + half * N_TILE) // N_TILE
+            bias_ps = banks.tile([P, N_TILE], F32, name="bias_ps", tag="bank")
+            nc.tensor.matmul(out=bias_ps[:], lhsT=bias_selector(gate, half), rhs=bias_rows[:], start=True, stop=True)
+            nc.vector.tensor_copy(out=bias_all[:, j, :], in_=bias_ps[:])
+
+        def add_bias(gate, half):
+            j = (GATE_COLUMN[gate] + half * N_TILE) // N_TILE
+            z = keep.tile([P, M_TILES, N_TILE], F32, name="z_%s%d" % (gate, half))
+            gate_values[gate, half] = z
+            for m in range(TENSOR_M_TILES):
+                z_ps = banks.tile([P, N_TILE], F32, name="z_ps", tag="bank")
+                nc.tensor.matmul(out=z_ps[:], lhsT=ident_bf16[:], rhs=xg_sb[gate, half][:, m, :], start=True, stop=False)
+                nc.tensor.matmul(out=z_ps[:], lhsT=bias_selector(gate, half), rhs=bias_rows[:], start=False, stop=True)
+                nc.scalar.copy(out=z[:, m, :], in_=z_ps[:])
+            for m in range(TENSOR_M_TILES, M_TILES):
+                nc.gpsimd.tensor_tensor(
+                    out=z[:, m, :], in0=xg_sb[gate, half][:, m, :], in1=bias_all[:, j, :], op=ADD
+                )
 
         quantised = {}
 
@@ -160,35 +151,51 @@ def tile_ircnn_lstmcell_pa_kernel(
             codes = keep.tile([P, M_TILES, K_GROUPS * P], U32, name="codes_" + key, align_bytes=64)
             scales = keep.tile([P, M_TILES, K_GROUPS * P], U8, name="scales_" + key, align_bytes=64)
             for m in range(M_TILES):
-                quantise_batch_tile(
-                    nc, psum_t, ident_f32, x_sb[:, m, :], grouped[:, m, :], codes[:, m, :], scales[:, m, :]
+                words = x_sb[:, m, :].bitcast(F32)
+                xt = banks.tile([P, K_GROUPS * 2, P], F32, name="xt", tag="bank")
+                for kg in range(K_GROUPS):
+                    for u in range(2):
+                        nc.tensor.transpose(
+                            xt[:, 2 * kg + u, :], words[:, 256 * kg + u : 256 * (kg + 1) : 2], ident_f32[:]
+                        )
+                nc.scalar.copy(
+                    out=grouped[:, m, :].bitcast(F32).rearrange("p (kg r u) -> p kg r u", kg=K_GROUPS, u=2),
+                    in_=xt[:].rearrange("p (kg u) r -> p kg r u", u=2),
+                )
+            if key == "hx":
+                for block in BLOCKS[3:]:
+                    spread_bias(*block)
+            for m in range(M_TILES):
+                nc.vector.quantize_mx(
+                    out=codes[:, m, :].bitcast(FP8X4), scales=scales[:, m, :], in_=grouped[:, m, :]
                 )
             quantised[key] = (codes, scales)
 
-        gate_values = {}
+        decay = keep.tile([P, 2 * M_TILES], F32, name="decay")
 
-        def compute_gate(name, half):
-            column = GATE_COLUMN[name] + half * N_TILE
-            z = keep.tile([P, M_TILES, N_TILE], F32, name="z_%s%d" % (name, half))
-            gate_values[name, half] = z
-            bias = bias_all[:, column // N_TILE, :].unsqueeze(1)
-            split = VECTOR_M_TILES
-            nc.vector.tensor_tensor(
-                out=z[:, 0:split, :], in0=xg_sb[name, half][:, 0:split, :],
-                in1=bias.to_broadcast([P, split, N_TILE]), op=ADD,
+        def decay_factors():
+            td_ps = banks.tile([P, P], BF16, name="td_ps", tag="bank")
+            nc.tensor.transpose(td_ps[:], td_rows[:], ident_bf16[:])
+            minus_b = keep.tile([P, 1], F32, name="minus_b")
+            nc.vector.tensor_scalar_mul(out=minus_b[:], in0=b_bf16[:], scalar1=-1.0)
+            a_f32 = keep.tile([P, 1], F32, name="a_f32")
+            nc.vector.tensor_copy(out=a_f32[:], in_=a_bf16[:])
+            nc.scalar.activation(
+                out=decay[:], in_=td_ps[:, 0 : 2 * M_TILES], func=FUNC.Exp, scale=minus_b[:, 0:1]
             )
-            nc.gpsimd.tensor_tensor(
-                out=z[:, split:M_TILES, :], in0=xg_sb[name, half][:, split:M_TILES, :],
-                in1=bias.to_broadcast([P, M_TILES - split, N_TILE]), op=ADD,
-            )
-            products = [("hx", hh_words[name, half], 0, column)]
-            if name != "g":
-                products.append(("cx", peep_words[name, half], 8, (0 if name == "i" else HID) + half * N_TILE))
+            nc.vector.tensor_scalar_mul(out=decay[:], in0=decay[:], scalar1=a_f32[:, 0:1])
+
+        def compute_gate(gate, half):
+            column = GATE_COLUMN[gate] + half * N_TILE
+            z = gate_values[gate, half]
+            products = [("hx", hh_words[gate, half], 0, column)]
+            if gate != "g":
+                products.append(("cx", peep_words[gate, half], 8, (0 if gate == "i" else HID) + half * N_TILE))
             last = len(products) * K_GROUPS - 1
             for m in range(M_TILES):
-                acc = psum_acc.tile([P, N_TILE], F32, name="acc")
+                acc = banks.tile([P, N_TILE], F32, name="acc", tag="bank")
                 count = 0
-                for key, words, first, plane_column in products:
+                for key, words, first_partition, plane_column in products:
                     codes, scales = quantised[key]
                     for kg in range(K_GROUPS):
                         nc.tensor.matmul_mx(
@@ -196,39 +203,50 @@ def tile_ircnn_lstmcell_pa_kernel(
                             lhsT=codes[:, m, kg * P : (kg + 1) * P].bitcast(FP8X4),
                             lhsT_scale=scales[:, m, kg * P : (kg + 1) * P],
                             rhs=words[:, kg, :].bitcast(FP8X4),
-                            rhs_scale=planes[first + 4 * kg : P, plane_column : plane_column + N_TILE],
+                            rhs_scale=planes[first_partition + 4 * kg : P, plane_column : plane_column + N_TILE],
                             start=(count == 0),
                             stop=(count == last),
                         )
                         count += 1
                 nc.vector.tensor_tensor(out=z[:, m, :], in0=acc[:], in1=z[:, m, :], op=ADD)
                 nc.scalar.activation(
-                    out=z[:, m, :], in_=z[:, m, :], func=FUNC.Tanh if name == "g" else FUNC.Sigmoid
+                    out=z[:, m, :], in_=z[:, m, :], func=FUNC.Tanh if gate == "g" else FUNC.Sigmoid
                 )
 
-        def combine(half):
-            columns = slice(half * N_TILE, (half + 1) * N_TILE)
+        def input_term(half):
             for m in range(M_TILES):
                 i_g = gate_values["i", half][:, m, :]
-                f_g = gate_values["f", half][:, m, :]
-                g_g = gate_values["g", half][:, m, :]
                 nc.vector.scalar_tensor_tensor(
-                    out=i_g, in0=i_g, scalar=decay[:, M_TILES + m : M_TILES + m + 1], in1=g_g, op0=MULT, op1=MULT
+                    out=i_g, in0=i_g, scalar=decay[:, M_TILES + m : M_TILES + m + 1],
+                    in1=gate_values["g", half][:, m, :], op0=MULT, op1=MULT,
                 )
+
+        def finish(half):
+            columns = slice(half * N_TILE, (half + 1) * N_TILE)
+            for m in range(M_TILES):
+                f_g = gate_values["f", half][:, m, :]
                 nc.vector.scalar_tensor_tensor(
                     out=f_g, in0=f_g, scalar=decay[:, m : m + 1], in1=cx_sb[:, m, columns], op0=MULT, op1=MULT
                 )
+            for m in range(M_TILES):
                 result = results.tile([P, N_TILE], F32, name="result")
-                nc.vector.tensor_tensor(out=result[:], in0=i_g, in1=f_g, op=ADD)
+                nc.vector.tensor_tensor(
+                    out=result[:], in0=gate_values["i", half][:, m, :], in1=gate_values["f", half][:, m, :], op=ADD
+                )
                 nc.sync.dma_start(out=out[m * P : (m + 1) * P, columns], in_=result[:])
 
+        for block in BLOCKS[:3]:
+            spread_bias(*block)
         quantise("hx", hx_sb)
-        compute_gate("g", 0)
-        quantise("cx", cx_sb)
-        compute_gate("i", 0)
-        compute_gate("f", 0)
-        combine(0)
-        compute_gate("g", 1)
-        compute_gate("i", 1)
-        compute_gate("f", 1)
-        combine(1)
+        add_bias(*BLOCKS[0])
+        decay_factors()
+        for step, (gate, half) in enumerate(BLOCKS):
+            if step + 1 < len(BLOCKS):
+                add_bias(*BLOCKS[step + 1])
+            compute_gate(gate, half)
+            if step == 1:
+                quantise("cx", cx_sb)
+            if gate == "i":
+                input_term(half)
+            if gate == "f":
+                finish(half)

@@ -23,7 +23,7 @@ N_TILE = 512
 HALVES = HID // N_TILE
 GATE_COLUMN = {"i": 0, "f": HID, "g": 2 * HID}
 BLOCKS = (("g", 0), ("g", 1), ("i", 0), ("f", 0), ("i", 1), ("f", 1))
-TENSOR_M_TILES = 2
+TENSOR_M_TILES = 1
 
 FLOPS = 2 * BATCH * HID * 5 * HID
 
@@ -51,12 +51,12 @@ def tile_ircnn_lstmcell_pa_kernel(
         ident_bf16 = keep.tile([P, P], BF16, name="ident_bf16")
         make_identity(nc, ident_bf16[:])
 
-        planes = keep.tile([P, 3 * HID], U8, name="planes", align_bytes=64)
-        nc.vector.memset(planes[:].bitcast(I32), 0)
         bias_rows = keep.tile([P, N_TILE], BF16, name="bias_rows")
         nc.vector.memset(bias_rows[:].bitcast(I32), 0)
         td_rows = keep.tile([P, P], BF16, name="td_rows")
         nc.vector.memset(td_rows[:].bitcast(I32), 0)
+        planes = keep.tile([P, 3 * HID], U8, name="planes", align_bytes=64)
+        nc.vector.memset(planes[:].bitcast(I32), 0)
 
         hx_sb = keep.tile([P, M_TILES, HID], BF16, name="hx_sb")
         cx_sb = keep.tile([P, M_TILES, HID], BF16, name="cx_sb")
@@ -102,7 +102,7 @@ def tile_ircnn_lstmcell_pa_kernel(
         load_scales(w_hh_scales, 0, 0, 3 * HID)
         load_xg(*BLOCKS[1])
         for step, block in enumerate(BLOCKS):
-            if step == 2:
+            if step == 1:
                 load_scales(w_pi_scales, 8, 0, HID)
                 load_scales(w_pf_scales, 8, HID, HID)
                 load_activations(cx_sb, cx)
@@ -110,12 +110,12 @@ def tile_ircnn_lstmcell_pa_kernel(
             if step + 2 < len(BLOCKS):
                 load_xg(*BLOCKS[step + 2])
 
-        nc.gpsimd.dma_start(out=td_rows[0:M_TILES, :], in_=td0.rearrange("(m p) -> m p", p=P))
-        nc.gpsimd.dma_start(out=td_rows[M_TILES : 2 * M_TILES, :], in_=td1.rearrange("(m p) -> m p", p=P))
+        nc.scalar.dma_start(out=td_rows[0:M_TILES, :], in_=td0.rearrange("(m p) -> m p", p=P))
+        nc.scalar.dma_start(out=td_rows[M_TILES : 2 * M_TILES, :], in_=td1.rearrange("(m p) -> m p", p=P))
         a_bf16 = keep.tile([P, 1], BF16, name="a_bf16")
-        nc.gpsimd.dma_start(out=a_bf16[:], in_=a.partition_broadcast(P))
+        nc.scalar.dma_start(out=a_bf16[:], in_=a.partition_broadcast(P))
         b_bf16 = keep.tile([P, 1], BF16, name="b_bf16")
-        nc.gpsimd.dma_start(out=b_bf16[:], in_=b.partition_broadcast(P))
+        nc.scalar.dma_start(out=b_bf16[:], in_=b.partition_broadcast(P))
 
         bias_all = keep.tile([P, 6, N_TILE], BF16, name="bias_all")
         gate_values = {}
@@ -162,12 +162,11 @@ def tile_ircnn_lstmcell_pa_kernel(
                     out=grouped[:, m, :].bitcast(F32).rearrange("p (kg r u) -> p kg r u", kg=K_GROUPS, u=2),
                     in_=xt[:].rearrange("p (kg u) r -> p kg r u", u=2),
                 )
-            if key == "hx":
-                for block in BLOCKS[3:]:
-                    spread_bias(*block)
-            for m in range(M_TILES):
+            for m in range(0, M_TILES, 2):
                 nc.vector.quantize_mx(
-                    out=codes[:, m, :].bitcast(FP8X4), scales=scales[:, m, :], in_=grouped[:, m, :]
+                    out=codes[:, m : m + 2, :].rearrange("p m w -> p (m w)").bitcast(FP8X4),
+                    scales=scales[:, m : m + 2, :].rearrange("p m w -> p (m w)"),
+                    in_=grouped[:, m : m + 2, :].rearrange("p m k -> p (m k)"),
                 )
             quantised[key] = (codes, scales)
 
@@ -238,13 +237,15 @@ def tile_ircnn_lstmcell_pa_kernel(
         for block in BLOCKS[:3]:
             spread_bias(*block)
         quantise("hx", hx_sb)
+        for block in BLOCKS[3:]:
+            spread_bias(*block)
         add_bias(*BLOCKS[0])
         decay_factors()
         for step, (gate, half) in enumerate(BLOCKS):
             if step + 1 < len(BLOCKS):
                 add_bias(*BLOCKS[step + 1])
             compute_gate(gate, half)
-            if step == 1:
+            if step == 0:
                 quantise("cx", cx_sb)
             if gate == "i":
                 input_term(half)

@@ -23,7 +23,7 @@ N_TILE = 512
 HALVES = HID // N_TILE
 GATE_COLUMN = {"i": 0, "f": HID, "g": 2 * HID}
 BLOCKS = (("g", 0), ("g", 1), ("i", 0), ("f", 0), ("i", 1), ("f", 1))
-TENSOR_M_TILES = 1
+GPSIMD_BLOCKS = (("g", 1), ("i", 0), ("f", 0))
 
 FLOPS = 2 * BATCH * HID * 5 * HID
 
@@ -51,12 +51,17 @@ def tile_ircnn_lstmcell_pa_kernel(
         ident_bf16 = keep.tile([P, P], BF16, name="ident_bf16")
         make_identity(nc, ident_bf16[:])
 
-        bias_rows = keep.tile([P, N_TILE], BF16, name="bias_rows")
-        nc.vector.memset(bias_rows[:].bitcast(I32), 0)
+        warm = keep.tile([P, 1], F32, name="warm")
+        nc.vector.memset(warm[:], 0.0)
         td_rows = keep.tile([P, P], BF16, name="td_rows")
         nc.vector.memset(td_rows[:].bitcast(I32), 0)
+        bias_rows = keep.tile([P, N_TILE], BF16, name="bias_rows")
+        nc.vector.memset(bias_rows[:].bitcast(I32), 0)
         planes = keep.tile([P, 3 * HID], U8, name="planes", align_bytes=64)
         nc.vector.memset(planes[:].bitcast(I32), 0)
+
+        def load_table(func):
+            nc.scalar.activation(out=warm[:], in_=warm[:], func=func)
 
         hx_sb = keep.tile([P, M_TILES, HID], BF16, name="hx_sb")
         cx_sb = keep.tile([P, M_TILES, HID], BF16, name="cx_sb")
@@ -65,10 +70,9 @@ def tile_ircnn_lstmcell_pa_kernel(
         peep_words = {}
         xg_by_tile = xg.rearrange("(m p) n -> p m n", p=P)
 
-        def load_activations(x_sb, x):
+        def load_activations(x_sb, x, m):
             by_tile = x.rearrange("(m p) k -> p m k", p=P)
-            for m in range(0, M_TILES, 2):
-                nc.sync.dma_start(out=x_sb[:, m : m + 2, :], in_=by_tile[:, m : m + 2, :])
+            nc.sync.dma_start(out=x_sb[:, m : m + 2, :], in_=by_tile[:, m : m + 2, :])
 
         def load_scales(scales_in, first_partition, first_column, width):
             for quad in range(4):
@@ -96,20 +100,28 @@ def tile_ircnn_lstmcell_pa_kernel(
                     nc, peep_words[gate, half], w_pi_words if gate == "i" else w_pf_words, half * N_TILE
                 )
 
+        load_activations(hx_sb, hx, 0)
         nc.sync.dma_start(out=bias_rows[0:6, :], in_=b_hh.rearrange("(j n) -> j n", n=N_TILE))
-        load_activations(hx_sb, hx)
-        load_xg(*BLOCKS[0])
+        load_activations(hx_sb, hx, 2)
+        load_xg("g", 0)
         load_scales(w_hh_scales, 0, 0, 3 * HID)
-        load_xg(*BLOCKS[1])
-        for step, block in enumerate(BLOCKS):
-            if step == 1:
-                load_scales(w_pi_scales, 8, 0, HID)
-                load_scales(w_pf_scales, 8, HID, HID)
-                load_activations(cx_sb, cx)
-            load_weights(*block)
-            if step + 2 < len(BLOCKS):
-                load_xg(*BLOCKS[step + 2])
+        load_weights("g", 0)
+        load_activations(cx_sb, cx, 0)
+        load_activations(cx_sb, cx, 2)
+        load_xg("g", 1)
+        load_weights("g", 1)
+        load_scales(w_pi_scales, 8, 0, HID)
+        load_scales(w_pf_scales, 8, HID, HID)
+        load_weights("i", 0)
+        load_xg("i", 0)
+        load_xg("f", 0)
+        load_weights("f", 0)
+        load_xg("i", 1)
+        load_weights("i", 1)
+        load_xg("f", 1)
+        load_weights("f", 1)
 
+        load_table(FUNC.Exp)
         nc.scalar.dma_start(out=td_rows[0:M_TILES, :], in_=td0.rearrange("(m p) -> m p", p=P))
         nc.scalar.dma_start(out=td_rows[M_TILES : 2 * M_TILES, :], in_=td1.rearrange("(m p) -> m p", p=P))
         a_bf16 = keep.tile([P, 1], BF16, name="a_bf16")
@@ -117,40 +129,46 @@ def tile_ircnn_lstmcell_pa_kernel(
         b_bf16 = keep.tile([P, 1], BF16, name="b_bf16")
         nc.scalar.dma_start(out=b_bf16[:], in_=b.partition_broadcast(P))
 
-        bias_all = keep.tile([P, 6, N_TILE], BF16, name="bias_all")
         gate_values = {}
+        for gate, half in BLOCKS:
+            gate_values[gate, half] = keep.tile([P, M_TILES, N_TILE], F32, name="z_%s%d" % (gate, half))
 
         def bias_selector(gate, half):
             j = (GATE_COLUMN[gate] + half * N_TILE) // N_TILE
             return ident_bf16[:, j : j + 1].to_broadcast([P, P])
 
+        bias_all = {}
+
         def spread_bias(gate, half):
-            j = (GATE_COLUMN[gate] + half * N_TILE) // N_TILE
             bias_ps = banks.tile([P, N_TILE], F32, name="bias_ps", tag="bank")
             nc.tensor.matmul(out=bias_ps[:], lhsT=bias_selector(gate, half), rhs=bias_rows[:], start=True, stop=True)
-            nc.vector.tensor_copy(out=bias_all[:, j, :], in_=bias_ps[:])
+            bias_all[gate, half] = keep.tile([P, N_TILE], BF16, name="bias_%s%d" % (gate, half))
+            nc.vector.tensor_copy(out=bias_all[gate, half][:], in_=bias_ps[:])
 
-        def add_bias(gate, half):
-            j = (GATE_COLUMN[gate] + half * N_TILE) // N_TILE
-            z = keep.tile([P, M_TILES, N_TILE], F32, name="z_%s%d" % (gate, half))
-            gate_values[gate, half] = z
-            for m in range(TENSOR_M_TILES):
-                z_ps = banks.tile([P, N_TILE], F32, name="z_ps", tag="bank")
-                nc.tensor.matmul(out=z_ps[:], lhsT=ident_bf16[:], rhs=xg_sb[gate, half][:, m, :], start=True, stop=False)
-                nc.tensor.matmul(out=z_ps[:], lhsT=bias_selector(gate, half), rhs=bias_rows[:], start=False, stop=True)
-                nc.scalar.copy(out=z[:, m, :], in_=z_ps[:])
-            for m in range(TENSOR_M_TILES, M_TILES):
+        def add_bias_gpsimd(gate, half):
+            for m in range(M_TILES):
                 nc.gpsimd.tensor_tensor(
-                    out=z[:, m, :], in0=xg_sb[gate, half][:, m, :], in1=bias_all[:, j, :], op=ADD
+                    out=gate_values[gate, half][:, m, :],
+                    in0=xg_sb[gate, half][:, m, :], in1=bias_all[gate, half][:], op=ADD,
                 )
 
-        quantised = {}
+        def add_bias_tensor(gate, half, m):
+            z_ps = banks.tile([P, N_TILE], F32, name="z_ps", tag="bank")
+            nc.tensor.matmul(out=z_ps[:], lhsT=ident_bf16[:], rhs=xg_sb[gate, half][:, m, :], start=True, stop=False)
+            nc.tensor.matmul(out=z_ps[:], lhsT=bias_selector(gate, half), rhs=bias_rows[:], start=False, stop=True)
+            nc.scalar.copy(out=gate_values[gate, half][:, m, :], in_=z_ps[:])
 
-        def quantise(key, x_sb):
-            grouped = keep.tile([P, M_TILES, HID], BF16, name="grouped_" + key, align_bytes=64)
-            codes = keep.tile([P, M_TILES, K_GROUPS * P], U32, name="codes_" + key, align_bytes=64)
-            scales = keep.tile([P, M_TILES, K_GROUPS * P], U8, name="scales_" + key, align_bytes=64)
-            for m in range(M_TILES):
+        quantised = {}
+        grouped_tiles = {}
+
+        def transpose_pair(key, x_sb, first_m):
+            if first_m == 0:
+                grouped_tiles[key] = keep.tile([P, M_TILES, HID], BF16, name="grouped_" + key, align_bytes=64)
+                codes = keep.tile([P, M_TILES, K_GROUPS * P], U32, name="codes_" + key, align_bytes=64)
+                scales = keep.tile([P, M_TILES, K_GROUPS * P], U8, name="scales_" + key, align_bytes=64)
+                quantised[key] = (codes, scales)
+            grouped = grouped_tiles[key]
+            for m in range(first_m, first_m + 2):
                 words = x_sb[:, m, :].bitcast(F32)
                 xt = banks.tile([P, K_GROUPS * 2, P], F32, name="xt", tag="bank")
                 for kg in range(K_GROUPS):
@@ -162,92 +180,103 @@ def tile_ircnn_lstmcell_pa_kernel(
                     out=grouped[:, m, :].bitcast(F32).rearrange("p (kg r u) -> p kg r u", kg=K_GROUPS, u=2),
                     in_=xt[:].rearrange("p (kg u) r -> p kg r u", u=2),
                 )
-            for m in range(0, M_TILES, 2):
-                nc.vector.quantize_mx(
-                    out=codes[:, m : m + 2, :].rearrange("p m w -> p (m w)").bitcast(FP8X4),
-                    scales=scales[:, m : m + 2, :].rearrange("p m w -> p (m w)"),
-                    in_=grouped[:, m : m + 2, :].rearrange("p m k -> p (m k)"),
-                )
-            quantised[key] = (codes, scales)
+
+        def quantise_pair(key, m):
+            codes, scales = quantised[key]
+            nc.vector.quantize_mx(
+                out=codes[:, m : m + 2, :].rearrange("p m w -> p (m w)").bitcast(FP8X4),
+                scales=scales[:, m : m + 2, :].rearrange("p m w -> p (m w)"),
+                in_=grouped_tiles[key][:, m : m + 2, :].rearrange("p m k -> p (m k)"),
+            )
 
         decay = keep.tile([P, 2 * M_TILES], F32, name="decay")
+        minus_b = keep.tile([P, 1], F32, name="minus_b")
+        a_f32 = keep.tile([P, 1], F32, name="a_f32")
 
-        def decay_factors():
+        def turn_time_gaps():
             td_ps = banks.tile([P, P], BF16, name="td_ps", tag="bank")
             nc.tensor.transpose(td_ps[:], td_rows[:], ident_bf16[:])
-            minus_b = keep.tile([P, 1], F32, name="minus_b")
+            nc.vector.tensor_copy(out=decay[:], in_=td_ps[:, 0 : 2 * M_TILES])
             nc.vector.tensor_scalar_mul(out=minus_b[:], in0=b_bf16[:], scalar1=-1.0)
-            a_f32 = keep.tile([P, 1], F32, name="a_f32")
             nc.vector.tensor_copy(out=a_f32[:], in_=a_bf16[:])
-            nc.scalar.activation(
-                out=decay[:], in_=td_ps[:, 0 : 2 * M_TILES], func=FUNC.Exp, scale=minus_b[:, 0:1]
-            )
+
+        def decay_factors():
+            nc.scalar.activation(out=decay[:], in_=decay[:], func=FUNC.Exp, scale=minus_b[:, 0:1])
             nc.vector.tensor_scalar_mul(out=decay[:], in0=decay[:], scalar1=a_f32[:, 0:1])
 
-        def compute_gate(gate, half):
+        def multiply(gate, half, m):
             column = GATE_COLUMN[gate] + half * N_TILE
             z = gate_values[gate, half]
             products = [("hx", hh_words[gate, half], 0, column)]
             if gate != "g":
                 products.append(("cx", peep_words[gate, half], 8, (0 if gate == "i" else HID) + half * N_TILE))
             last = len(products) * K_GROUPS - 1
-            for m in range(M_TILES):
-                acc = banks.tile([P, N_TILE], F32, name="acc", tag="bank")
-                count = 0
-                for key, words, first_partition, plane_column in products:
-                    codes, scales = quantised[key]
-                    for kg in range(K_GROUPS):
-                        nc.tensor.matmul_mx(
-                            out=acc[:],
-                            lhsT=codes[:, m, kg * P : (kg + 1) * P].bitcast(FP8X4),
-                            lhsT_scale=scales[:, m, kg * P : (kg + 1) * P],
-                            rhs=words[:, kg, :].bitcast(FP8X4),
-                            rhs_scale=planes[first_partition + 4 * kg : P, plane_column : plane_column + N_TILE],
-                            start=(count == 0),
-                            stop=(count == last),
-                        )
-                        count += 1
-                nc.vector.tensor_tensor(out=z[:, m, :], in0=acc[:], in1=z[:, m, :], op=ADD)
-                nc.scalar.activation(
-                    out=z[:, m, :], in_=z[:, m, :], func=FUNC.Tanh if gate == "g" else FUNC.Sigmoid
-                )
+            acc = banks.tile([P, N_TILE], F32, name="acc", tag="bank")
+            count = 0
+            for key, words, first_partition, plane_column in products:
+                codes, scales = quantised[key]
+                for kg in range(K_GROUPS):
+                    nc.tensor.matmul_mx(
+                        out=acc[:],
+                        lhsT=codes[:, m, kg * P : (kg + 1) * P].bitcast(FP8X4),
+                        lhsT_scale=scales[:, m, kg * P : (kg + 1) * P],
+                        rhs=words[:, kg, :].bitcast(FP8X4),
+                        rhs_scale=planes[first_partition + 4 * kg : P, plane_column : plane_column + N_TILE],
+                        start=(count == 0),
+                        stop=(count == last),
+                    )
+                    count += 1
+            nc.vector.tensor_tensor(out=z[:, m, :], in0=acc[:], in1=z[:, m, :], op=ADD)
+            nc.scalar.activation(out=z[:, m, :], in_=z[:, m, :], func=FUNC.Tanh if gate == "g" else FUNC.Sigmoid)
 
-        def input_term(half):
-            for m in range(M_TILES):
-                i_g = gate_values["i", half][:, m, :]
-                nc.vector.scalar_tensor_tensor(
-                    out=i_g, in0=i_g, scalar=decay[:, M_TILES + m : M_TILES + m + 1],
-                    in1=gate_values["g", half][:, m, :], op0=MULT, op1=MULT,
-                )
-
-        def finish(half):
-            columns = slice(half * N_TILE, (half + 1) * N_TILE)
-            for m in range(M_TILES):
-                f_g = gate_values["f", half][:, m, :]
-                nc.vector.scalar_tensor_tensor(
-                    out=f_g, in0=f_g, scalar=decay[:, m : m + 1], in1=cx_sb[:, m, columns], op0=MULT, op1=MULT
-                )
-            for m in range(M_TILES):
-                result = results.tile([P, N_TILE], F32, name="result")
-                nc.vector.tensor_tensor(
-                    out=result[:], in0=gate_values["i", half][:, m, :], in1=gate_values["f", half][:, m, :], op=ADD
-                )
-                nc.sync.dma_start(out=out[m * P : (m + 1) * P, columns], in_=result[:])
-
-        for block in BLOCKS[:3]:
-            spread_bias(*block)
-        quantise("hx", hx_sb)
-        for block in BLOCKS[3:]:
-            spread_bias(*block)
-        add_bias(*BLOCKS[0])
-        decay_factors()
-        for step, (gate, half) in enumerate(BLOCKS):
-            if step + 1 < len(BLOCKS):
-                add_bias(*BLOCKS[step + 1])
-            compute_gate(gate, half)
-            if step == 0:
-                quantise("cx", cx_sb)
-            if gate == "i":
-                input_term(half)
+        def product(gate, half, m):
+            value = gate_values[gate, half][:, m, :]
+            factor_column = m if gate == "f" else M_TILES + m
             if gate == "f":
-                finish(half)
+                other = cx_sb[:, m, half * N_TILE : (half + 1) * N_TILE]
+            else:
+                other = gate_values["g", half][:, m, :]
+            nc.vector.scalar_tensor_tensor(
+                out=value, in0=value, scalar=decay[:, factor_column : factor_column + 1], in1=other, op0=MULT, op1=MULT
+            )
+
+        def finish(half, m):
+            result = results.tile([P, N_TILE], F32, name="result")
+            nc.vector.tensor_tensor(
+                out=result[:], in0=gate_values["i", half][:, m, :], in1=gate_values["f", half][:, m, :], op=ADD
+            )
+            nc.sync.dma_start(
+                out=out[m * P : (m + 1) * P, half * N_TILE : (half + 1) * N_TILE], in_=result[:]
+            )
+
+        transpose_pair("hx", hx_sb, 0)
+        for block in GPSIMD_BLOCKS:
+            spread_bias(*block)
+        transpose_pair("hx", hx_sb, 2)
+        turn_time_gaps()
+        quantise_pair("hx", 0)
+        quantise_pair("hx", 2)
+        for m in range(M_TILES):
+            add_bias_tensor("g", 0, m)
+        for block in GPSIMD_BLOCKS:
+            add_bias_gpsimd(*block)
+
+        steps = [(gate, half, m) for gate, half in BLOCKS for m in range(M_TILES)]
+        next_tensor_block = {("f", 0): ("i", 1), ("i", 1): ("f", 1)}
+        for s in range(len(steps) + 2):
+            if s < len(steps):
+                gate, half, m = steps[s]
+                multiply(gate, half, m)
+                if (gate, half) in next_tensor_block:
+                    add_bias_tensor(*next_tensor_block[gate, half], m)
+            if 1 <= s <= len(steps) and steps[s - 1][0] != "g":
+                product(*steps[s - 1])
+            if s >= 2 and steps[s - 2][0] == "f":
+                finish(*steps[s - 2][1:])
+            if s == M_TILES - 1:
+                for m in range(0, M_TILES, 2):
+                    transpose_pair("cx", cx_sb, m)
+                    quantise_pair("cx", m)
+            if s == 2 * M_TILES - 1:
+                decay_factors()
+                load_table(FUNC.Sigmoid)

@@ -25,6 +25,8 @@ GATE_COLUMN = {"i": 0, "f": HID, "g": 2 * HID}
 BLOCKS = (("g", 0), ("g", 1), ("i", 0), ("f", 0), ("i", 1), ("f", 1))
 GPSIMD_BLOCKS = (("g", 1), ("i", 0), ("f", 0))
 
+B_COLUMN = 16
+
 FLOPS = 2 * BATCH * HID * 5 * HID
 
 
@@ -124,10 +126,8 @@ def tile_ircnn_lstmcell_pa_kernel(
         load_table(FUNC.Exp)
         nc.scalar.dma_start(out=td_rows[0:M_TILES, :], in_=td0.rearrange("(m p) -> m p", p=P))
         nc.scalar.dma_start(out=td_rows[M_TILES : 2 * M_TILES, :], in_=td1.rearrange("(m p) -> m p", p=P))
-        a_bf16 = keep.tile([P, 1], BF16, name="a_bf16")
-        nc.scalar.dma_start(out=a_bf16[:], in_=a.partition_broadcast(P))
-        b_bf16 = keep.tile([P, 1], BF16, name="b_bf16")
-        nc.scalar.dma_start(out=b_bf16[:], in_=b.partition_broadcast(P))
+        nc.scalar.dma_start(out=bias_rows[6:7, 0:1], in_=a.rearrange("(j n) -> j n", n=1))
+        nc.scalar.dma_start(out=bias_rows[6:7, B_COLUMN : B_COLUMN + 1], in_=b.rearrange("(j n) -> j n", n=1))
 
         gate_values = {}
         for gate, half in BLOCKS:
@@ -197,8 +197,13 @@ def tile_ircnn_lstmcell_pa_kernel(
             td_ps = banks.tile([P, P], BF16, name="td_ps", tag="bank")
             nc.tensor.transpose(td_ps[:], td_rows[:], ident_bf16[:])
             nc.vector.tensor_copy(out=decay[:], in_=td_ps[:, 0 : 2 * M_TILES])
-            nc.vector.tensor_scalar_mul(out=minus_b[:], in0=b_bf16[:], scalar1=-1.0)
-            nc.vector.tensor_copy(out=a_f32[:], in_=a_bf16[:])
+            ab_ps = banks.tile([P, 2 * B_COLUMN], F32, name="ab_ps", tag="bank")
+            nc.tensor.matmul(
+                out=ab_ps[:], lhsT=ident_bf16[:, 6:7].to_broadcast([P, P]), rhs=bias_rows[:, 0 : 2 * B_COLUMN],
+                start=True, stop=True,
+            )
+            nc.vector.tensor_copy(out=a_f32[:], in_=ab_ps[:, 0:1])
+            nc.vector.tensor_scalar_mul(out=minus_b[:], in0=ab_ps[:, B_COLUMN : B_COLUMN + 1], scalar1=-1.0)
 
         def decay_factors():
             nc.scalar.activation(out=decay[:], in_=decay[:], func=FUNC.Exp, scale=minus_b[:, 0:1])

@@ -57,9 +57,9 @@ def tile_ircnn_lstmcell_pa_kernel(
         nc.vector.memset(warm[:], 0.0)
         td_rows = keep.tile([P, P], BF16, name="td_rows")
         nc.vector.memset(td_rows[:].bitcast(I32), 0)
-        bias_rows = keep.tile([P, N_TILE], BF16, name="bias_rows")
+        bias_rows = keep.tile([P, 3 * N_TILE], BF16, name="bias_rows")
         nc.vector.memset(bias_rows[:].bitcast(I32), 0)
-        planes = keep.tile([P, 3 * HID], U8, name="planes", align_bytes=64)
+        planes = keep.tile([P, K_GROUPS, 3 * HID], U8, name="planes", align_bytes=64)
         nc.vector.memset(planes[:].bitcast(I32), 0)
 
         def load_table(func):
@@ -76,13 +76,12 @@ def tile_ircnn_lstmcell_pa_kernel(
             by_tile = x.rearrange("(m p) k -> p m k", p=P)
             nc.sync.dma_start(out=x_sb[:, m : m + 2, :], in_=by_tile[:, m : m + 2, :])
 
-        def load_scales(scales_in, first_partition, first_column, width):
-            for quad in range(4):
-                start = 32 * quad + first_partition
-                nc.sync.dma_start(
-                    out=planes[start : start + 8, first_column : first_column + width].bitcast(I32),
-                    in_=scales_in[:, 4 * quad : 4 * quad + 4, :].bitcast(I32),
-                )
+        def load_scales(scales_in, first_partition, first_column, width, row):
+            columns = planes[:, :, first_column : first_column + width].bitcast(I32)
+            nc.sync.dma_start(
+                out=columns[first_partition + row : P : 32, :, :],
+                in_=scales_in.bitcast(I32).rearrange("kg (q r) n -> r q kg n", r=4)[row],
+            )
 
         def load_xg(gate, half):
             column = GATE_COLUMN[gate] + half * N_TILE
@@ -103,17 +102,24 @@ def tile_ircnn_lstmcell_pa_kernel(
                 )
 
         load_activations(hx_sb, hx, 0)
-        nc.sync.dma_start(out=bias_rows[0:6, :], in_=b_hh.rearrange("(j n) -> j n", n=N_TILE))
+        nc.sync.dma_start(out=bias_rows[0:2, :], in_=b_hh.rearrange("(j n) -> j n", n=3 * N_TILE))
         load_activations(hx_sb, hx, 2)
         load_xg("g", 0)
-        load_scales(w_hh_scales, 0, 0, 3 * HID)
+        for row in range(4):
+            load_scales(w_hh_scales, 0, 0, 3 * HID, row)
         load_weights("g", 0)
         load_activations(cx_sb, cx, 0)
+        load_scales(w_pi_scales, 8, 0, HID, 0)
+        load_scales(w_pi_scales, 8, 0, HID, 1)
         load_activations(cx_sb, cx, 2)
+        load_scales(w_pi_scales, 8, 0, HID, 2)
+        load_scales(w_pi_scales, 8, 0, HID, 3)
         load_xg("g", 1)
+        load_scales(w_pf_scales, 8, HID, HID, 0)
+        load_scales(w_pf_scales, 8, HID, HID, 1)
         load_weights("g", 1)
-        load_scales(w_pi_scales, 8, 0, HID)
-        load_scales(w_pf_scales, 8, HID, HID)
+        load_scales(w_pf_scales, 8, HID, HID, 2)
+        load_scales(w_pf_scales, 8, HID, HID, 3)
         load_weights("i", 0)
         load_xg("i", 0)
         load_xg("f", 0)
@@ -134,14 +140,14 @@ def tile_ircnn_lstmcell_pa_kernel(
             gate_values[gate, half] = keep.tile([P, M_TILES, N_TILE], F32, name="z_%s%d" % (gate, half))
 
         def bias_selector(gate, half):
-            j = (GATE_COLUMN[gate] + half * N_TILE) // N_TILE
-            return ident_bf16[:, j : j + 1].to_broadcast([P, P])
+            j, column = divmod(GATE_COLUMN[gate] + half * N_TILE, 3 * N_TILE)
+            return {"lhsT": ident_bf16[:, j : j + 1].to_broadcast([P, P]), "rhs": bias_rows[:, column : column + N_TILE]}
 
         bias_all = {}
 
         def spread_bias(gate, half):
             bias_ps = banks.tile([P, N_TILE], F32, name="bias_ps", tag="bank")
-            nc.tensor.matmul(out=bias_ps[:], lhsT=bias_selector(gate, half), rhs=bias_rows[:], start=True, stop=True)
+            nc.tensor.matmul(out=bias_ps[:], **bias_selector(gate, half), start=True, stop=True)
             bias_all[gate, half] = keep.tile([P, N_TILE], BF16, name="bias_%s%d" % (gate, half))
             nc.vector.tensor_copy(out=bias_all[gate, half][:], in_=bias_ps[:])
 
@@ -155,7 +161,7 @@ def tile_ircnn_lstmcell_pa_kernel(
         def add_bias_tensor(gate, half, m):
             z_ps = banks.tile([P, N_TILE], F32, name="z_ps", tag="bank")
             nc.tensor.matmul(out=z_ps[:], lhsT=ident_bf16[:], rhs=xg_sb[gate, half][:, m, :], start=True, stop=False)
-            nc.tensor.matmul(out=z_ps[:], lhsT=bias_selector(gate, half), rhs=bias_rows[:], start=False, stop=True)
+            nc.tensor.matmul(out=z_ps[:], **bias_selector(gate, half), start=False, stop=True)
             nc.scalar.copy(out=gate_values[gate, half][:, m, :], in_=z_ps[:])
 
         quantised = {}
@@ -212,13 +218,13 @@ def tile_ircnn_lstmcell_pa_kernel(
         def multiply(gate, half, m):
             column = GATE_COLUMN[gate] + half * N_TILE
             z = gate_values[gate, half]
-            products = [("hx", hh_words[gate, half], 0, column)]
+            products = [("hx", hh_words[gate, half], 0)]
             if gate != "g":
-                products.append(("cx", peep_words[gate, half], 8, (0 if gate == "i" else HID) + half * N_TILE))
+                products.append(("cx", peep_words[gate, half], 8))
             last = len(products) * K_GROUPS - 1
             acc = banks.tile([P, N_TILE], F32, name="acc", tag="bank")
             count = 0
-            for key, words, first_partition, plane_column in products:
+            for key, words, first_partition in products:
                 codes, scales = quantised[key]
                 for kg in range(K_GROUPS):
                     nc.tensor.matmul_mx(
@@ -226,7 +232,7 @@ def tile_ircnn_lstmcell_pa_kernel(
                         lhsT=codes[:, m, kg * P : (kg + 1) * P].bitcast(FP8X4),
                         lhsT_scale=scales[:, m, kg * P : (kg + 1) * P],
                         rhs=words[:, kg, :].bitcast(FP8X4),
-                        rhs_scale=planes[first_partition + 4 * kg : P, plane_column : plane_column + N_TILE],
+                        rhs_scale=planes[first_partition:P, kg, column : column + N_TILE],
                         start=(count == 0),
                         stop=(count == last),
                     )

@@ -23,7 +23,7 @@ N_TILE = 512
 HALVES = HID // N_TILE
 GATE_COLUMN = {"i": 0, "f": HID, "g": 2 * HID}
 BLOCKS = (("g", 0), ("g", 1), ("i", 0), ("f", 0), ("i", 1), ("f", 1))
-GPSIMD_BLOCKS = (("g", 1), ("i", 0), ("f", 0))
+BIAS_ENGINE = {("g", 0): "tttt", ("g", 1): "gggg", ("i", 0): "gggg", ("f", 0): "gggg", ("i", 1): "tttt", ("f", 1): "tttt"}
 
 B_COLUMN = 16
 
@@ -59,8 +59,10 @@ def tile_ircnn_lstmcell_pa_kernel(
         nc.vector.memset(td_rows[:].bitcast(I32), 0)
         bias_rows = keep.tile([P, 3 * N_TILE], BF16, name="bias_rows")
         nc.vector.memset(bias_rows[:].bitcast(I32), 0)
-        planes = keep.tile([P, K_GROUPS, 3 * HID], U8, name="planes", align_bytes=64)
-        nc.vector.memset(planes[:].bitcast(I32), 0)
+        planes_g = keep.tile([P, K_GROUPS, HID], U8, name="planes_g", align_bytes=64)
+        planes_if = keep.tile([P, K_GROUPS, 2 * HID], U8, name="planes_if", align_bytes=64)
+        nc.vector.memset(planes_g[:].bitcast(I32), 0)
+        nc.vector.memset(planes_if[:].bitcast(I32), 0)
 
         def load_table(func):
             nc.scalar.activation(out=warm[:], in_=warm[:], func=func)
@@ -76,12 +78,24 @@ def tile_ircnn_lstmcell_pa_kernel(
             by_tile = x.rearrange("(m p) k -> p m k", p=P)
             nc.sync.dma_start(out=x_sb[:, m : m + 2, :], in_=by_tile[:, m : m + 2, :])
 
-        def load_scales(scales_in, first_partition, first_column, width, row):
-            columns = planes[:, :, first_column : first_column + width].bitcast(I32)
+        def load_scales(planes, first_partition, first_column, scales_in, source_column, width, row):
+            rows = scales_in.rearrange("kg (q r) n -> r q kg n", r=4)[row]
             nc.sync.dma_start(
-                out=columns[first_partition + row : P : 32, :, :],
-                in_=scales_in.bitcast(I32).rearrange("kg (q r) n -> r q kg n", r=4)[row],
+                out=planes[first_partition + row : P : 32, :, first_column : first_column + width].bitcast(I32),
+                in_=rows[:, :, source_column : source_column + width].bitcast(I32),
             )
+
+        def load_scales_g(row):
+            load_scales(planes_g, 0, 0, w_hh_scales, 2 * HID, HID, row)
+
+        def load_scales_if(row):
+            load_scales(planes_if, 0, 0, w_hh_scales, 0, 2 * HID, row)
+
+        def load_scales_pi(row):
+            load_scales(planes_if, 8, 0, w_pi_scales, 0, HID, row)
+
+        def load_scales_pf(row):
+            load_scales(planes_if, 8, HID, w_pf_scales, 0, HID, row)
 
         def load_xg(gate, half):
             column = GATE_COLUMN[gate] + half * N_TILE
@@ -106,29 +120,26 @@ def tile_ircnn_lstmcell_pa_kernel(
         load_activations(hx_sb, hx, 2)
         load_xg("g", 0)
         for row in range(4):
-            load_scales(w_hh_scales, 0, 0, 3 * HID, row)
+            load_scales_g(row)
         load_weights("g", 0)
         load_activations(cx_sb, cx, 0)
-        load_scales(w_pi_scales, 8, 0, HID, 0)
-        load_scales(w_pi_scales, 8, 0, HID, 1)
+        for row in range(4):
+            load_scales_if(row)
         load_activations(cx_sb, cx, 2)
-        load_scales(w_pi_scales, 8, 0, HID, 2)
-        load_scales(w_pi_scales, 8, 0, HID, 3)
+        for row in range(4):
+            load_scales_pi(row)
         load_xg("g", 1)
-        load_scales(w_pf_scales, 8, HID, HID, 0)
-        load_scales(w_pf_scales, 8, HID, HID, 1)
+        for row in range(4):
+            load_scales_pf(row)
         load_weights("g", 1)
-        load_scales(w_pf_scales, 8, HID, HID, 2)
-        load_scales(w_pf_scales, 8, HID, HID, 3)
-        load_weights("i", 0)
         load_xg("i", 0)
+        load_weights("i", 0)
         load_xg("f", 0)
         load_weights("f", 0)
         load_xg("i", 1)
         load_weights("i", 1)
         load_xg("f", 1)
         load_weights("f", 1)
-
         load_table(FUNC.Exp)
         nc.scalar.dma_start(out=td_rows[0:M_TILES, :], in_=td0.rearrange("(m p) -> m p", p=P))
         nc.scalar.dma_start(out=td_rows[M_TILES : 2 * M_TILES, :], in_=td1.rearrange("(m p) -> m p", p=P))
@@ -151,12 +162,11 @@ def tile_ircnn_lstmcell_pa_kernel(
             bias_all[gate, half] = keep.tile([P, N_TILE], BF16, name="bias_%s%d" % (gate, half))
             nc.vector.tensor_copy(out=bias_all[gate, half][:], in_=bias_ps[:])
 
-        def add_bias_gpsimd(gate, half):
-            for m in range(M_TILES):
-                nc.gpsimd.tensor_tensor(
-                    out=gate_values[gate, half][:, m, :],
-                    in0=xg_sb[gate, half][:, m, :], in1=bias_all[gate, half][:], op=ADD,
-                )
+        def add_bias(engine, gate, half, m):
+            engine.tensor_tensor(
+                out=gate_values[gate, half][:, m, :],
+                in0=xg_sb[gate, half][:, m, :], in1=bias_all[gate, half][:], op=ADD,
+            )
 
         def add_bias_tensor(gate, half, m):
             z_ps = banks.tile([P, N_TILE], F32, name="z_ps", tag="bank")
@@ -216,7 +226,8 @@ def tile_ircnn_lstmcell_pa_kernel(
             nc.vector.tensor_scalar_mul(out=decay[:], in0=decay[:], scalar1=a_f32[:, 0:1])
 
         def multiply(gate, half, m):
-            column = GATE_COLUMN[gate] + half * N_TILE
+            column = half * N_TILE if gate == "g" else GATE_COLUMN[gate] + half * N_TILE
+            planes = planes_g if gate == "g" else planes_if
             z = gate_values[gate, half]
             products = [("hx", hh_words[gate, half], 0)]
             if gate != "g":
@@ -260,34 +271,43 @@ def tile_ircnn_lstmcell_pa_kernel(
                 out=out[m * P : (m + 1) * P, half * N_TILE : (half + 1) * N_TILE], in_=result[:]
             )
 
-        transpose_pair("hx", hx_sb, 0)
-        for block in GPSIMD_BLOCKS:
-            spread_bias(*block)
-        transpose_pair("hx", hx_sb, 2)
+        def bias_tiles(gate, half, who):
+            return [m for m in range(M_TILES) if BIAS_ENGINE[gate, half][m] == who]
+
+        for block in BLOCKS:
+            if BIAS_ENGINE[block] != "tttt":
+                spread_bias(*block)
+        for m in range(0, M_TILES, 2):
+            transpose_pair("hx", hx_sb, m)
         turn_time_gaps()
-        quantise_pair("hx", 0)
-        quantise_pair("hx", 2)
-        for m in range(M_TILES):
-            add_bias_tensor("g", 0, m)
-        for block in GPSIMD_BLOCKS:
-            add_bias_gpsimd(*block)
+        for m in range(0, M_TILES, 2):
+            quantise_pair("hx", m)
+        decay_factors()
+        load_table(FUNC.Sigmoid)
+        for block in BLOCKS:
+            for m in bias_tiles(*block, "g"):
+                add_bias(nc.gpsimd, *block, m)
 
         steps = [(gate, half, m) for gate, half in BLOCKS for m in range(M_TILES)]
-        next_tensor_block = {("f", 0): ("i", 1), ("i", 1): ("f", 1)}
-        for s in range(len(steps) + 2):
+        for m in bias_tiles(*BLOCKS[0], "t"):
+            add_bias_tensor(*BLOCKS[0], m)
+        for s in range(len(steps) + 3):
             if s < len(steps):
                 gate, half, m = steps[s]
+                if m == 0:
+                    for tile in bias_tiles(gate, half, "v"):
+                        add_bias(nc.vector, gate, half, tile)
                 multiply(gate, half, m)
-                if (gate, half) in next_tensor_block:
-                    add_bias_tensor(*next_tensor_block[gate, half], m)
-            if 1 <= s <= len(steps) and steps[s - 1][0] != "g":
-                product(*steps[s - 1])
-            if s >= 2 and steps[s - 2][0] == "f":
-                finish(*steps[s - 2][1:])
-            if s == M_TILES - 1:
+                if s + M_TILES < len(steps):
+                    ahead = steps[s + M_TILES]
+                    if ahead[2] in bias_tiles(*ahead[:2], "t"):
+                        add_bias_tensor(*ahead)
+            if 2 <= s < len(steps) + 2 and steps[s - 2][0] != "g":
+                product(*steps[s - 2])
+            if s >= 3 and steps[s - 3][0] == "f":
+                finish(*steps[s - 3][1:])
+            if s == 3:
                 for m in range(0, M_TILES, 2):
                     transpose_pair("cx", cx_sb, m)
-                    quantise_pair("cx", m)
-            if s == 2 * M_TILES - 1:
-                decay_factors()
-                load_table(FUNC.Sigmoid)
+            if s in (4, 5):
+                quantise_pair("cx", 0 if s == 4 else 2)

@@ -22,9 +22,10 @@ K_GROUPS = HID // K_PASS
 N_TILE = 512
 HALVES = HID // N_TILE
 GATE_COLUMN = {"i": 0, "f": HID, "g": 2 * HID}
-BLOCKS = (("g", 0), ("g", 1), ("i", 0), ("f", 0), ("i", 1), ("f", 1))
-BIAS_ENGINE = {("g", 0): "tttt", ("g", 1): "gggg", ("i", 0): "gggg", ("f", 0): "gggg", ("i", 1): "tttt", ("f", 1): "tttt"}
+BLOCKS = (("g", 0), ("i", 0), ("g", 1), ("f", 0), ("i", 1), ("f", 1))
+BIAS_ENGINE = {("g", 0): "gggg", ("i", 0): "vvgg", ("g", 1): "ggtt", ("f", 0): "gggg", ("i", 1): "ggtt", ("f", 1): "tttt"}
 
+A_COLUMN = 3 * N_TILE
 B_COLUMN = 16
 
 FLOPS = 2 * BATCH * HID * 5 * HID
@@ -55,9 +56,8 @@ def tile_ircnn_lstmcell_pa_kernel(
 
         warm = keep.tile([P, 1], F32, name="warm")
         nc.vector.memset(warm[:], 0.0)
-        td_rows = keep.tile([P, P], BF16, name="td_rows")
-        nc.vector.memset(td_rows[:].bitcast(I32), 0)
-        bias_rows = keep.tile([P, 3 * N_TILE], BF16, name="bias_rows")
+        td_sb = keep.tile([P, 2, 16], BF16, name="td_sb")
+        bias_rows = keep.tile([P, 3 * N_TILE + 2 * B_COLUMN], BF16, name="bias_rows")
         nc.vector.memset(bias_rows[:].bitcast(I32), 0)
         planes_g = keep.tile([P, K_GROUPS, HID], U8, name="planes_g", align_bytes=64)
         planes_if = keep.tile([P, K_GROUPS, 2 * HID], U8, name="planes_if", align_bytes=64)
@@ -72,10 +72,11 @@ def tile_ircnn_lstmcell_pa_kernel(
         xg_sb = {}
         hh_words = {}
         peep_words = {}
-        xg_by_tile = xg.rearrange("(m p) n -> p m n", p=P)
+        xg_by_tile = xg.rearrange("(p m) n -> p m n", p=P)
+        out_by_tile = out.rearrange("(p m) n -> p m n", p=P)
 
         def load_activations(x_sb, x, m):
-            by_tile = x.rearrange("(m p) k -> p m k", p=P)
+            by_tile = x.rearrange("(p m) k -> p m k", p=P)
             nc.sync.dma_start(out=x_sb[:, m : m + 2, :], in_=by_tile[:, m : m + 2, :])
 
         def load_scales(planes, first_partition, first_column, scales_in, source_column, width, row):
@@ -116,24 +117,24 @@ def tile_ircnn_lstmcell_pa_kernel(
                 )
 
         load_activations(hx_sb, hx, 0)
-        nc.sync.dma_start(out=bias_rows[0:2, :], in_=b_hh.rearrange("(j n) -> j n", n=3 * N_TILE))
+        nc.sync.dma_start(out=bias_rows[0:2, 0 : 3 * N_TILE], in_=b_hh.rearrange("(j n) -> j n", n=3 * N_TILE))
+        for row in range(4):
+            load_scales_g(row)
         load_activations(hx_sb, hx, 2)
         load_xg("g", 0)
         for row in range(4):
-            load_scales_g(row)
-        load_weights("g", 0)
-        load_activations(cx_sb, cx, 0)
-        for row in range(4):
             load_scales_if(row)
+        load_activations(cx_sb, cx, 0)
         load_activations(cx_sb, cx, 2)
         for row in range(4):
             load_scales_pi(row)
-        load_xg("g", 1)
-        for row in range(4):
-            load_scales_pf(row)
-        load_weights("g", 1)
+        load_weights("g", 0)
         load_xg("i", 0)
         load_weights("i", 0)
+        for row in range(4):
+            load_scales_pf(row)
+        load_xg("g", 1)
+        load_weights("g", 1)
         load_xg("f", 0)
         load_weights("f", 0)
         load_xg("i", 1)
@@ -141,10 +142,16 @@ def tile_ircnn_lstmcell_pa_kernel(
         load_xg("f", 1)
         load_weights("f", 1)
         load_table(FUNC.Exp)
-        nc.scalar.dma_start(out=td_rows[0:M_TILES, :], in_=td0.rearrange("(m p) -> m p", p=P))
-        nc.scalar.dma_start(out=td_rows[M_TILES : 2 * M_TILES, :], in_=td1.rearrange("(m p) -> m p", p=P))
-        nc.scalar.dma_start(out=bias_rows[6:7, 0:1], in_=a.rearrange("(j n) -> j n", n=1))
-        nc.scalar.dma_start(out=bias_rows[6:7, B_COLUMN : B_COLUMN + 1], in_=b.rearrange("(j n) -> j n", n=1))
+        nc.scalar.dma_start(out=td_sb[:, 0, 0:M_TILES], in_=td0.rearrange("(p m) -> p m", p=P))
+        nc.scalar.dma_start(out=td_sb[:, 1, 0:M_TILES], in_=td1.rearrange("(p m) -> p m", p=P))
+        nc.scalar.dma_start(out=bias_rows[0:1, A_COLUMN : A_COLUMN + 1], in_=a.rearrange("(j n) -> j n", n=1))
+        nc.scalar.dma_start(
+            out=bias_rows[0:1, A_COLUMN + B_COLUMN : A_COLUMN + B_COLUMN + 1], in_=b.rearrange("(j n) -> j n", n=1)
+        )
+
+        selectors = keep.tile([P, 2, P], BF16, name="selectors")
+        for j in range(2):
+            nc.vector.tensor_copy(out=selectors[:, j, :], in_=ident_bf16[:, j : j + 1].to_broadcast([P, P]))
 
         gate_values = {}
         for gate, half in BLOCKS:
@@ -152,7 +159,7 @@ def tile_ircnn_lstmcell_pa_kernel(
 
         def bias_selector(gate, half):
             j, column = divmod(GATE_COLUMN[gate] + half * N_TILE, 3 * N_TILE)
-            return {"lhsT": ident_bf16[:, j : j + 1].to_broadcast([P, P]), "rhs": bias_rows[:, column : column + N_TILE]}
+            return {"lhsT": selectors[:, j, :], "rhs": bias_rows[:, column : column + N_TILE]}
 
         bias_all = {}
 
@@ -160,13 +167,16 @@ def tile_ircnn_lstmcell_pa_kernel(
             bias_ps = banks.tile([P, N_TILE], F32, name="bias_ps", tag="bank")
             nc.tensor.matmul(out=bias_ps[:], **bias_selector(gate, half), start=True, stop=True)
             bias_all[gate, half] = keep.tile([P, N_TILE], BF16, name="bias_%s%d" % (gate, half))
-            nc.vector.tensor_copy(out=bias_all[gate, half][:], in_=bias_ps[:])
+            nc.scalar.copy(out=bias_all[gate, half][:], in_=bias_ps[:])
 
         def add_bias(engine, gate, half, m):
-            engine.tensor_tensor(
-                out=gate_values[gate, half][:, m, :],
-                in0=xg_sb[gate, half][:, m, :], in1=bias_all[gate, half][:], op=ADD,
-            )
+            pieces = 2 if engine is nc.gpsimd else 1
+            for piece in range(pieces):
+                columns = slice(piece * N_TILE // pieces, (piece + 1) * N_TILE // pieces)
+                engine.tensor_tensor(
+                    out=gate_values[gate, half][:, m, columns],
+                    in0=xg_sb[gate, half][:, m, columns], in1=bias_all[gate, half][:, columns], op=ADD,
+                )
 
         def add_bias_tensor(gate, half, m):
             z_ps = banks.tile([P, N_TILE], F32, name="z_ps", tag="bank")
@@ -177,25 +187,23 @@ def tile_ircnn_lstmcell_pa_kernel(
         quantised = {}
         grouped_tiles = {}
 
-        def transpose_pair(key, x_sb, first_m):
-            if first_m == 0:
+        def transpose_tile(key, x_sb, m):
+            if m == 0:
                 grouped_tiles[key] = keep.tile([P, M_TILES, HID], BF16, name="grouped_" + key, align_bytes=64)
                 codes = keep.tile([P, M_TILES, K_GROUPS * P], U32, name="codes_" + key, align_bytes=64)
                 scales = keep.tile([P, M_TILES, K_GROUPS * P], U8, name="scales_" + key, align_bytes=64)
                 quantised[key] = (codes, scales)
-            grouped = grouped_tiles[key]
-            for m in range(first_m, first_m + 2):
-                words = x_sb[:, m, :].bitcast(F32)
-                xt = banks.tile([P, K_GROUPS * 2, P], F32, name="xt", tag="bank")
-                for kg in range(K_GROUPS):
-                    for u in range(2):
-                        nc.tensor.transpose(
-                            xt[:, 2 * kg + u, :], words[:, 256 * kg + u : 256 * (kg + 1) : 2], ident_f32[:]
-                        )
-                nc.scalar.copy(
-                    out=grouped[:, m, :].bitcast(F32).rearrange("p (kg r u) -> p kg r u", kg=K_GROUPS, u=2),
-                    in_=xt[:].rearrange("p (kg u) r -> p kg r u", u=2),
-                )
+            words = x_sb[:, m, :].bitcast(F32)
+            xt = banks.tile([P, K_GROUPS * 2, P], F32, name="xt", tag="bank")
+            for kg in range(K_GROUPS):
+                for u in range(2):
+                    nc.tensor.transpose(
+                        xt[:, 2 * kg + u, :], words[:, 256 * kg + u : 256 * (kg + 1) : 2], ident_f32[:]
+                    )
+            nc.scalar.copy(
+                out=grouped_tiles[key][:, m, :].bitcast(F32).rearrange("p (kg r u) -> p kg r u", kg=K_GROUPS, u=2),
+                in_=xt[:].rearrange("p (kg u) r -> p kg r u", u=2),
+            )
 
         def quantise_pair(key, m):
             codes, scales = quantised[key]
@@ -209,26 +217,25 @@ def tile_ircnn_lstmcell_pa_kernel(
         minus_b = keep.tile([P, 1], F32, name="minus_b")
         a_f32 = keep.tile([P, 1], F32, name="a_f32")
 
-        def turn_time_gaps():
-            td_ps = banks.tile([P, P], BF16, name="td_ps", tag="bank")
-            nc.tensor.transpose(td_ps[:], td_rows[:], ident_bf16[:])
-            nc.vector.tensor_copy(out=decay[:], in_=td_ps[:, 0 : 2 * M_TILES])
+        def spread_a_and_b():
             ab_ps = banks.tile([P, 2 * B_COLUMN], F32, name="ab_ps", tag="bank")
             nc.tensor.matmul(
-                out=ab_ps[:], lhsT=ident_bf16[:, 6:7].to_broadcast([P, P]), rhs=bias_rows[:, 0 : 2 * B_COLUMN],
+                out=ab_ps[:], lhsT=selectors[:, 0, :], rhs=bias_rows[:, A_COLUMN : A_COLUMN + 2 * B_COLUMN],
                 start=True, stop=True,
             )
             nc.vector.tensor_copy(out=a_f32[:], in_=ab_ps[:, 0:1])
             nc.vector.tensor_scalar_mul(out=minus_b[:], in0=ab_ps[:, B_COLUMN : B_COLUMN + 1], scalar1=-1.0)
 
         def decay_factors():
-            nc.scalar.activation(out=decay[:], in_=decay[:], func=FUNC.Exp, scale=minus_b[:, 0:1])
+            nc.scalar.activation(
+                out=decay[:].rearrange("p (j m) -> p j m", j=2), in_=td_sb[:, :, 0:M_TILES], func=FUNC.Exp, scale=minus_b[:, 0:1]
+            )
             nc.vector.tensor_scalar_mul(out=decay[:], in0=decay[:], scalar1=a_f32[:, 0:1])
 
-        def multiply(gate, half, m):
-            column = half * N_TILE if gate == "g" else GATE_COLUMN[gate] + half * N_TILE
+        def multiply(gate, half, m, first, width):
+            column = first + (half * N_TILE if gate == "g" else GATE_COLUMN[gate] + half * N_TILE)
             planes = planes_g if gate == "g" else planes_if
-            z = gate_values[gate, half]
+            z = gate_values[gate, half][:, m, first : first + width]
             products = [("hx", hh_words[gate, half], 0)]
             if gate != "g":
                 products.append(("cx", peep_words[gate, half], 8))
@@ -239,75 +246,79 @@ def tile_ircnn_lstmcell_pa_kernel(
                 codes, scales = quantised[key]
                 for kg in range(K_GROUPS):
                     nc.tensor.matmul_mx(
-                        out=acc[:],
+                        out=acc[:, 0:width],
                         lhsT=codes[:, m, kg * P : (kg + 1) * P].bitcast(FP8X4),
                         lhsT_scale=scales[:, m, kg * P : (kg + 1) * P],
-                        rhs=words[:, kg, :].bitcast(FP8X4),
-                        rhs_scale=planes[first_partition:P, kg, column : column + N_TILE],
+                        rhs=words[:, kg, first : first + width].bitcast(FP8X4),
+                        rhs_scale=planes[first_partition:P, kg, column : column + width],
                         start=(count == 0),
                         stop=(count == last),
                     )
                     count += 1
-            nc.vector.tensor_tensor(out=z[:, m, :], in0=acc[:], in1=z[:, m, :], op=ADD)
-            nc.scalar.activation(out=z[:, m, :], in_=z[:, m, :], func=FUNC.Tanh if gate == "g" else FUNC.Sigmoid)
+            nc.vector.tensor_tensor(out=z, in0=acc[:, 0:width], in1=z, op=ADD)
+            nc.scalar.activation(out=z, in_=z, func=FUNC.Tanh if gate == "g" else FUNC.Sigmoid)
 
-        def product(gate, half, m):
-            value = gate_values[gate, half][:, m, :]
+        def product(gate, half, m, first, width):
+            value = gate_values[gate, half][:, m, first : first + width]
             factor_column = m if gate == "f" else M_TILES + m
             if gate == "f":
-                other = cx_sb[:, m, half * N_TILE : (half + 1) * N_TILE]
+                other = cx_sb[:, m, half * N_TILE + first : half * N_TILE + first + width]
             else:
-                other = gate_values["g", half][:, m, :]
+                other = gate_values["g", half][:, m, first : first + width]
             nc.vector.scalar_tensor_tensor(
                 out=value, in0=value, scalar=decay[:, factor_column : factor_column + 1], in1=other, op0=MULT, op1=MULT
             )
 
-        def finish(half, m):
+        def finish(gate, half, m, first, width):
             result = results.tile([P, N_TILE], F32, name="result")
             nc.vector.tensor_tensor(
-                out=result[:], in0=gate_values["i", half][:, m, :], in1=gate_values["f", half][:, m, :], op=ADD
+                out=result[:, 0:width],
+                in0=gate_values["i", half][:, m, first : first + width],
+                in1=gate_values[gate, half][:, m, first : first + width],
+                op=ADD,
             )
-            nc.sync.dma_start(
-                out=out[m * P : (m + 1) * P, half * N_TILE : (half + 1) * N_TILE], in_=result[:]
-            )
+            column = half * N_TILE + first
+            nc.sync.dma_start(out=out_by_tile[:, m, column : column + width], in_=result[:, 0:width])
 
         def bias_tiles(gate, half, who):
             return [m for m in range(M_TILES) if BIAS_ENGINE[gate, half][m] == who]
 
-        for block in BLOCKS:
-            if BIAS_ENGINE[block] != "tttt":
+        spread = [block for block in BLOCKS if BIAS_ENGINE[block] != "tttt"]
+        for m in range(M_TILES):
+            transpose_tile("hx", hx_sb, m)
+            if m % 2:
+                quantise_pair("hx", m - 1)
+            for block in spread[m:: M_TILES]:
                 spread_bias(*block)
-        for m in range(0, M_TILES, 2):
-            transpose_pair("hx", hx_sb, m)
-        turn_time_gaps()
-        for m in range(0, M_TILES, 2):
-            quantise_pair("hx", m)
+        spread_a_and_b()
+        for m in range(M_TILES):
+            transpose_tile("cx", cx_sb, m)
+            if m % 2:
+                quantise_pair("cx", m - 1)
         decay_factors()
         load_table(FUNC.Sigmoid)
         for block in BLOCKS:
             for m in bias_tiles(*block, "g"):
                 add_bias(nc.gpsimd, *block, m)
 
-        steps = [(gate, half, m) for gate, half in BLOCKS for m in range(M_TILES)]
+        steps = [(gate, half, m, 0, N_TILE) for gate, half in BLOCKS for m in range(M_TILES)]
+        gate, half, m, first, width = steps.pop()
+        for piece in range(1):
+            steps.append((gate, half, m, piece * N_TILE // 1, N_TILE // 1))
         for m in bias_tiles(*BLOCKS[0], "t"):
             add_bias_tensor(*BLOCKS[0], m)
         for s in range(len(steps) + 3):
             if s < len(steps):
-                gate, half, m = steps[s]
+                gate, half, m, first, width = steps[s]
                 if m == 0:
                     for tile in bias_tiles(gate, half, "v"):
                         add_bias(nc.vector, gate, half, tile)
-                multiply(gate, half, m)
-                if s + M_TILES < len(steps):
-                    ahead = steps[s + M_TILES]
+                multiply(*steps[s])
+                if s + M_TILES < len(steps) and steps[s + M_TILES][3] == 0:
+                    ahead = steps[s + M_TILES][:3]
                     if ahead[2] in bias_tiles(*ahead[:2], "t"):
                         add_bias_tensor(*ahead)
             if 2 <= s < len(steps) + 2 and steps[s - 2][0] != "g":
                 product(*steps[s - 2])
             if s >= 3 and steps[s - 3][0] == "f":
-                finish(*steps[s - 3][1:])
-            if s == 3:
-                for m in range(0, M_TILES, 2):
-                    transpose_pair("cx", cx_sb, m)
-            if s in (4, 5):
-                quantise_pair("cx", 0 if s == 4 else 2)
+                finish(*steps[s - 3])

@@ -23,7 +23,7 @@ N_TILE = 512
 HALVES = HID // N_TILE
 GATE_COLUMN = {"i": 0, "f": HID, "g": 2 * HID}
 BLOCKS = (("g", 0), ("i", 0), ("g", 1), ("f", 0), ("i", 1), ("f", 1))
-BIAS_ENGINE = {("g", 0): "gggg", ("i", 0): "vvgg", ("g", 1): "ggtt", ("f", 0): "gggg", ("i", 1): "ggtt", ("f", 1): "tttt"}
+BIAS_ENGINE = {("g", 0): "gggg", ("i", 0): "vvtt", ("g", 1): "ggtt", ("f", 0): "gggg", ("i", 1): "ggtt", ("f", 1): "tttt"}
 
 A_COLUMN = 3 * N_TILE
 B_COLUMN = 16
@@ -170,13 +170,10 @@ def tile_ircnn_lstmcell_pa_kernel(
             nc.scalar.copy(out=bias_all[gate, half][:], in_=bias_ps[:])
 
         def add_bias(engine, gate, half, m):
-            pieces = 2 if engine is nc.gpsimd else 1
-            for piece in range(pieces):
-                columns = slice(piece * N_TILE // pieces, (piece + 1) * N_TILE // pieces)
-                engine.tensor_tensor(
-                    out=gate_values[gate, half][:, m, columns],
-                    in0=xg_sb[gate, half][:, m, columns], in1=bias_all[gate, half][:, columns], op=ADD,
-                )
+            engine.tensor_tensor(
+                out=gate_values[gate, half][:, m, :],
+                in0=xg_sb[gate, half][:, m, :], in1=bias_all[gate, half][:], op=ADD,
+            )
 
         def add_bias_tensor(gate, half, m):
             z_ps = banks.tile([P, N_TILE], F32, name="z_ps", tag="bank")

@@ -59,10 +59,10 @@ def tile_ircnn_lstmcell_pa_kernel(
         td_sb = keep.tile([P, 2, 16], BF16, name="td_sb")
         bias_rows = keep.tile([P, 3 * N_TILE + 2 * B_COLUMN], BF16, name="bias_rows")
         nc.vector.memset(bias_rows[:].bitcast(I32), 0)
-        planes_g = keep.tile([P, K_GROUPS, HID], U8, name="planes_g", align_bytes=64)
-        planes_if = keep.tile([P, K_GROUPS, 2 * HID], U8, name="planes_if", align_bytes=64)
-        nc.vector.memset(planes_g[:].bitcast(I32), 0)
-        nc.vector.memset(planes_if[:].bitcast(I32), 0)
+        planes_hh = keep.tile([P, K_GROUPS, 3 * HID], U8, name="planes_hh", align_bytes=64)
+        planes_peep = keep.tile([P, K_GROUPS, 2 * HID], U8, name="planes_peep", align_bytes=64)
+        nc.vector.memset(planes_hh[:].bitcast(I32), 0)
+        nc.vector.memset(planes_peep[:].bitcast(I32), 0)
 
         def load_table(func):
             nc.scalar.activation(out=warm[:], in_=warm[:], func=func)
@@ -79,24 +79,21 @@ def tile_ircnn_lstmcell_pa_kernel(
             by_tile = x.rearrange("(p m) k -> p m k", p=P)
             nc.sync.dma_start(out=x_sb[:, m : m + 2, :], in_=by_tile[:, m : m + 2, :])
 
-        def load_scales(planes, first_partition, first_column, scales_in, source_column, width, row):
-            rows = scales_in.rearrange("kg (q r) n -> r q kg n", r=4)[row]
+        def load_scales(planes, first_column, scales_in, row):
+            width = scales_in.shape[2]
             nc.sync.dma_start(
-                out=planes[first_partition + row : P : 32, :, first_column : first_column + width].bitcast(I32),
-                in_=rows[:, :, source_column : source_column + width].bitcast(I32),
+                out=planes[row : P : 32, :, first_column : first_column + width].bitcast(I32),
+                in_=scales_in.rearrange("kg (q r) n -> r q kg n", r=4)[row].bitcast(I32),
             )
 
-        def load_scales_g(row):
-            load_scales(planes_g, 0, 0, w_hh_scales, 2 * HID, HID, row)
-
-        def load_scales_if(row):
-            load_scales(planes_if, 0, 0, w_hh_scales, 0, 2 * HID, row)
+        def load_scales_hh(row):
+            load_scales(planes_hh, 0, w_hh_scales, row)
 
         def load_scales_pi(row):
-            load_scales(planes_if, 8, 0, w_pi_scales, 0, HID, row)
+            load_scales(planes_peep, 0, w_pi_scales, row)
 
         def load_scales_pf(row):
-            load_scales(planes_if, 8, HID, w_pf_scales, 0, HID, row)
+            load_scales(planes_peep, HID, w_pf_scales, row)
 
         def load_xg(gate, half):
             column = GATE_COLUMN[gate] + half * N_TILE
@@ -117,13 +114,11 @@ def tile_ircnn_lstmcell_pa_kernel(
                 )
 
         load_activations(hx_sb, hx, 0)
-        nc.sync.dma_start(out=bias_rows[0:2, 0 : 3 * N_TILE], in_=b_hh.rearrange("(j n) -> j n", n=3 * N_TILE))
-        for row in range(4):
-            load_scales_g(row)
         load_activations(hx_sb, hx, 2)
+        nc.sync.dma_start(out=bias_rows[0:2, 0 : 3 * N_TILE], in_=b_hh.rearrange("(j n) -> j n", n=3 * N_TILE))
         load_xg("g", 0)
         for row in range(4):
-            load_scales_if(row)
+            load_scales_hh(row)
         load_activations(cx_sb, cx, 0)
         load_activations(cx_sb, cx, 2)
         for row in range(4):
@@ -141,13 +136,14 @@ def tile_ircnn_lstmcell_pa_kernel(
         load_weights("i", 1)
         load_xg("f", 1)
         load_weights("f", 1)
-        load_table(FUNC.Exp)
         nc.scalar.dma_start(out=td_sb[:, 0, 0:M_TILES], in_=td0.rearrange("(p m) -> p m", p=P))
         nc.scalar.dma_start(out=td_sb[:, 1, 0:M_TILES], in_=td1.rearrange("(p m) -> p m", p=P))
         nc.scalar.dma_start(out=bias_rows[0:1, A_COLUMN : A_COLUMN + 1], in_=a.rearrange("(j n) -> j n", n=1))
         nc.scalar.dma_start(
             out=bias_rows[0:1, A_COLUMN + B_COLUMN : A_COLUMN + B_COLUMN + 1], in_=b.rearrange("(j n) -> j n", n=1)
         )
+
+        load_table(FUNC.Exp)
 
         selectors = keep.tile([P, 2, P], BF16, name="selectors")
         for j in range(2):
@@ -230,16 +226,15 @@ def tile_ircnn_lstmcell_pa_kernel(
             nc.vector.tensor_scalar_mul(out=decay[:], in0=decay[:], scalar1=a_f32[:, 0:1])
 
         def multiply(gate, half, m, first, width):
-            column = first + (half * N_TILE if gate == "g" else GATE_COLUMN[gate] + half * N_TILE)
-            planes = planes_g if gate == "g" else planes_if
+            column = GATE_COLUMN[gate] + half * N_TILE + first
             z = gate_values[gate, half][:, m, first : first + width]
-            products = [("hx", hh_words[gate, half], 0)]
+            products = [("hx", hh_words[gate, half], planes_hh)]
             if gate != "g":
-                products.append(("cx", peep_words[gate, half], 8))
+                products.append(("cx", peep_words[gate, half], planes_peep))
             last = len(products) * K_GROUPS - 1
             acc = banks.tile([P, N_TILE], F32, name="acc", tag="bank")
             count = 0
-            for key, words, first_partition in products:
+            for key, words, planes in products:
                 codes, scales = quantised[key]
                 for kg in range(K_GROUPS):
                     nc.tensor.matmul_mx(
@@ -247,7 +242,7 @@ def tile_ircnn_lstmcell_pa_kernel(
                         lhsT=codes[:, m, kg * P : (kg + 1) * P].bitcast(FP8X4),
                         lhsT_scale=scales[:, m, kg * P : (kg + 1) * P],
                         rhs=words[:, kg, first : first + width].bitcast(FP8X4),
-                        rhs_scale=planes[first_partition:P, kg, column : column + width],
+                        rhs_scale=planes[:, kg, column : column + width],
                         start=(count == 0),
                         stop=(count == last),
                     )

@@ -117,13 +117,13 @@ def tile_ircnn_lstmcell_pa_kernel(
         load_activations(hx_sb, hx, 2)
         nc.sync.dma_start(out=bias_rows[0:2, 0 : 3 * N_TILE], in_=b_hh.rearrange("(j n) -> j n", n=3 * N_TILE))
         load_xg("g", 0)
+        load_activations(cx_sb, cx, 0)
         for row in range(4):
             load_scales_hh(row)
-        load_activations(cx_sb, cx, 0)
         load_activations(cx_sb, cx, 2)
+        load_weights("g", 0)
         for row in range(4):
             load_scales_pi(row)
-        load_weights("g", 0)
         load_xg("i", 0)
         load_weights("i", 0)
         for row in range(4):
@@ -295,8 +295,8 @@ def tile_ircnn_lstmcell_pa_kernel(
 
         steps = [(gate, half, m, 0, N_TILE) for gate, half in BLOCKS for m in range(M_TILES)]
         gate, half, m, first, width = steps.pop()
-        for piece in range(1):
-            steps.append((gate, half, m, piece * N_TILE // 1, N_TILE // 1))
+        for piece in range(2):
+            steps.append((gate, half, m, piece * N_TILE // 2, N_TILE // 2))
         for m in bias_tiles(*BLOCKS[0], "t"):
             add_bias_tensor(*BLOCKS[0], m)
         for s in range(len(steps) + 3):

from contextlib import ExitStack

import concourse.mybir as mybir
from concourse.masks import make_identity

F32 = mybir.dt.float32
BF16 = mybir.dt.bfloat16
I32 = mybir.dt.int32
U32 = mybir.dt.uint32
U8 = mybir.dt.uint8
FP8X4 = mybir.dt.float8_e4m3fn_x4
ADD = mybir.AluOpType.add
MULT = mybir.AluOpType.mult
FUNC = mybir.ActivationFunctionType

P = 128
BATCH = 512
HID = 1024
M_TILES = BATCH // P
K_PASS = 512
K_GROUPS = HID // K_PASS
N_TILE = 512
HALVES = HID // N_TILE
GATE_COLUMN = {"i": 0, "f": HID, "g": 2 * HID}
BLOCKS = (("g", 0), ("i", 0), ("g", 1), ("f", 0), ("i", 1), ("f", 1))
BIAS_ENGINE = {("g", 0): "gggg", ("i", 0): "vvtt", ("g", 1): "ggtt", ("f", 0): "gggg", ("i", 1): "ggtt", ("f", 1): "tttt"}

A_COLUMN = 3 * N_TILE
B_COLUMN = 16

FLOPS = 2 * BATCH * HID * 5 * HID


def load_weight_words(nc, words_tile, words, first_column):
    by_partition = words.rearrange("kg p n t -> p kg (n t)")
    columns = by_partition[:, :, 4 * first_column : 4 * (first_column + N_TILE)]
    nc.sync.dma_start(out=words_tile[:].bitcast(I32), in_=columns.bitcast(I32))


def tile_ircnn_lstmcell_pa_kernel(
    tc, xg, hx, cx, td0, td1,
    w_hh_words, w_hh_scales, w_pi_words, w_pi_scales, w_pf_words, w_pf_scales,
    b_hh, a, b, out,
):
    nc = tc.nc
    with ExitStack() as ctx:
        keep = ctx.enter_context(tc.tile_pool(name="keep", bufs=1))
        results = ctx.enter_context(tc.tile_pool(name="results", bufs=4))
        banks = ctx.enter_context(tc.psum_pool(name="banks", bufs=8))
        ctx.enter_context(tc.manual_schedule())

        ident_f32 = keep.tile([P, P], F32, name="ident_f32")
        make_identity(nc, ident_f32[:])
        ident_bf16 = keep.tile([P, P], BF16, name="ident_bf16")
        make_identity(nc, ident_bf16[:])

        warm = keep.tile([P, 1], F32, name="warm")
        nc.vector.memset(warm[:], 0.0)
        td_sb = keep.tile([P, 2, 16], BF16, name="td_sb")
        bias_rows = keep.tile([P, 3 * N_TILE + 2 * B_COLUMN], BF16, name="bias_rows")
        nc.vector.memset(bias_rows[:].bitcast(I32), 0)
        planes_hh = keep.tile([P, K_GROUPS, 3 * HID], U8, name="planes_hh", align_bytes=64)
        planes_peep = keep.tile([P, K_GROUPS, 2 * HID], U8, name="planes_peep", align_bytes=64)
        nc.vector.memset(planes_hh[:].bitcast(I32), 0)
        nc.vector.memset(planes_peep[:].bitcast(I32), 0)

        def load_table(func):
            nc.scalar.activation(out=warm[:], in_=warm[:], func=func)

        hx_sb = keep.tile([P, M_TILES, HID], BF16, name="hx_sb")
        cx_sb = keep.tile([P, M_TILES, HID], BF16, name="cx_sb")
        xg_sb = {}
        hh_words = {}
        peep_words = {}
        xg_by_tile = xg.rearrange("(p m) n -> p m n", p=P)
        out_by_tile = out.rearrange("(p m) n -> p m n", p=P)

        def load_activations(x_sb, x, m):
            by_tile = x.rearrange("(p m) k -> p m k", p=P)
            nc.sync.dma_start(out=x_sb[:, m : m + 2, :], in_=by_tile[:, m : m + 2, :])

        def load_scales(planes, first_column, scales_in, row):
            width = scales_in.shape[2]
            nc.sync.dma_start(
                out=planes[row : P : 32, :, first_column : first_column + width].bitcast(I32),
                in_=scales_in.rearrange("kg (q r) n -> r q kg n", r=4)[row].bitcast(I32),
            )

        def load_scales_hh(row):
            load_scales(planes_hh, 0, w_hh_scales, row)

        def load_scales_pi(row):
            load_scales(planes_peep, 0, w_pi_scales, row)

        def load_scales_pf(row):
            load_scales(planes_peep, HID, w_pf_scales, row)

        def load_xg(gate, half):
            column = GATE_COLUMN[gate] + half * N_TILE
            xg_sb[gate, half] = keep.tile([P, M_TILES, N_TILE], BF16, name="xg_%s%d" % (gate, half))
            nc.sync.dma_start(out=xg_sb[gate, half][:], in_=xg_by_tile[:, :, column : column + N_TILE])

        def load_weights(gate, half):
            hh_words[gate, half] = keep.tile(
                [P, K_GROUPS, N_TILE], U32, name="hh_%s%d" % (gate, half), align_bytes=64
            )
            load_weight_words(nc, hh_words[gate, half], w_hh_words, GATE_COLUMN[gate] + half * N_TILE)
            if gate != "g":
                peep_words[gate, half] = keep.tile(
                    [P, K_GROUPS, N_TILE], U32, name="peep_%s%d" % (gate, half), align_bytes=64
                )
                load_weight_words(
                    nc, peep_words[gate, half], w_pi_words if gate == "i" else w_pf_words, half * N_TILE
                )

        load_activations(hx_sb, hx, 0)
        load_activations(hx_sb, hx, 2)
        nc.sync.dma_start(out=bias_rows[0:2, 0 : 3 * N_TILE], in_=b_hh.rearrange("(j n) -> j n", n=3 * N_TILE))
        load_xg("g", 0)
        load_activations(cx_sb, cx, 0)
        for row in range(4):
            load_scales_hh(row)
        load_activations(cx_sb, cx, 2)
        load_weights("g", 0)
        for row in range(4):
            load_scales_pi(row)
        load_xg("i", 0)
        load_weights("i", 0)
        for row in range(4):
            load_scales_pf(row)
        load_xg("g", 1)
        load_weights("g", 1)
        load_xg("f", 0)
        load_weights("f", 0)
        load_xg("i", 1)
        load_weights("i", 1)
        load_xg("f", 1)
        load_weights("f", 1)
        nc.scalar.dma_start(out=td_sb[:, 0, 0:M_TILES], in_=td0.rearrange("(p m) -> p m", p=P))
        nc.scalar.dma_start(out=td_sb[:, 1, 0:M_TILES], in_=td1.rearrange("(p m) -> p m", p=P))
        nc.scalar.dma_start(out=bias_rows[0:1, A_COLUMN : A_COLUMN + 1], in_=a.rearrange("(j n) -> j n", n=1))
        nc.scalar.dma_start(
            out=bias_rows[0:1, A_COLUMN + B_COLUMN : A_COLUMN + B_COLUMN + 1], in_=b.rearrange("(j n) -> j n", n=1)
        )

        load_table(FUNC.Exp)

        selectors = keep.tile([P, 2, P], BF16, name="selectors")
        for j in range(2):
            nc.vector.tensor_copy(out=selectors[:, j, :], in_=ident_bf16[:, j : j + 1].to_broadcast([P, P]))

        gate_values = {}
        for gate, half in BLOCKS:
            gate_values[gate, half] = keep.tile([P, M_TILES, N_TILE], F32, name="z_%s%d" % (gate, half))

        def bias_selector(gate, half):
            j, column = divmod(GATE_COLUMN[gate] + half * N_TILE, 3 * N_TILE)
            return {"lhsT": selectors[:, j, :], "rhs": bias_rows[:, column : column + N_TILE]}

        bias_all = {}

        def spread_bias(gate, half):
            bias_ps = banks.tile([P, N_TILE], F32, name="bias_ps", tag="bank")
            nc.tensor.matmul(out=bias_ps[:], **bias_selector(gate, half), start=True, stop=True)
            bias_all[gate, half] = keep.tile([P, N_TILE], BF16, name="bias_%s%d" % (gate, half))
            nc.scalar.copy(out=bias_all[gate, half][:], in_=bias_ps[:])

        def add_bias(engine, gate, half, m):
            engine.tensor_tensor(
                out=gate_values[gate, half][:, m, :],
                in0=xg_sb[gate, half][:, m, :], in1=bias_all[gate, half][:], op=ADD,
            )

        def add_bias_tensor(gate, half, m):
            z_ps = banks.tile([P, N_TILE], F32, name="z_ps", tag="bank")
            nc.tensor.matmul(out=z_ps[:], lhsT=ident_bf16[:], rhs=xg_sb[gate, half][:, m, :], start=True, stop=False)
            nc.tensor.matmul(out=z_ps[:], **bias_selector(gate, half), start=False, stop=True)
            nc.scalar.copy(out=gate_values[gate, half][:, m, :], in_=z_ps[:])

        quantised = {}
        grouped_tiles = {}

        def transpose_tile(key, x_sb, m):
            if m == 0:
                grouped_tiles[key] = keep.tile([P, M_TILES, HID], BF16, name="grouped_" + key, align_bytes=64)
                codes = keep.tile([P, M_TILES, K_GROUPS * P], U32, name="codes_" + key, align_bytes=64)
                scales = keep.tile([P, M_TILES, K_GROUPS * P], U8, name="scales_" + key, align_bytes=64)
                quantised[key] = (codes, scales)
            words = x_sb[:, m, :].bitcast(F32)
            xt = banks.tile([P, K_GROUPS * 2, P], F32, name="xt", tag="bank")
            for kg in range(K_GROUPS):
                for u in range(2):
                    nc.tensor.transpose(
                        xt[:, 2 * kg + u, :], words[:, 256 * kg + u : 256 * (kg + 1) : 2], ident_f32[:]
                    )
            nc.scalar.copy(
                out=grouped_tiles[key][:, m, :].bitcast(F32).rearrange("p (kg r u) -> p kg r u", kg=K_GROUPS, u=2),
                in_=xt[:].rearrange("p (kg u) r -> p kg r u", u=2),
            )

        def quantise_pair(key, m):
            codes, scales = quantised[key]
            nc.vector.quantize_mx(
                out=codes[:, m : m + 2, :].rearrange("p m w -> p (m w)").bitcast(FP8X4),
                scales=scales[:, m : m + 2, :].rearrange("p m w -> p (m w)"),
                in_=grouped_tiles[key][:, m : m + 2, :].rearrange("p m k -> p (m k)"),
            )

        decay = keep.tile([P, 2 * M_TILES], F32, name="decay")
        minus_b = keep.tile([P, 1], F32, name="minus_b")
        a_f32 = keep.tile([P, 1], F32, name="a_f32")

        def spread_a_and_b():
            ab_ps = banks.tile([P, 2 * B_COLUMN], F32, name="ab_ps", tag="bank")
            nc.tensor.matmul(
                out=ab_ps[:], lhsT=selectors[:, 0, :], rhs=bias_rows[:, A_COLUMN : A_COLUMN + 2 * B_COLUMN],
                start=True, stop=True,
            )
            nc.vector.tensor_copy(out=a_f32[:], in_=ab_ps[:, 0:1])
            nc.vector.tensor_scalar_mul(out=minus_b[:], in0=ab_ps[:, B_COLUMN : B_COLUMN + 1], scalar1=-1.0)

        def decay_factors():
            nc.scalar.activation(
                out=decay[:].rearrange("p (j m) -> p j m", j=2), in_=td_sb[:, :, 0:M_TILES], func=FUNC.Exp, scale=minus_b[:, 0:1]
            )
            nc.vector.tensor_scalar_mul(out=decay[:], in0=decay[:], scalar1=a_f32[:, 0:1])

        def multiply(gate, half, m, first, width):
            column = GATE_COLUMN[gate] + half * N_TILE + first
            z = gate_values[gate, half][:, m, first : first + width]
            products = [("hx", hh_words[gate, half], planes_hh)]
            if gate != "g":
                products.append(("cx", peep_words[gate, half], planes_peep))
            last = len(products) * K_GROUPS - 1
            acc = banks.tile([P, N_TILE], F32, name="acc", tag="bank")
            count = 0
            for key, words, planes in products:
                codes, scales = quantised[key]
                for kg in range(K_GROUPS):
                    nc.tensor.matmul_mx(
                        out=acc[:, 0:width],
                        lhsT=codes[:, m, kg * P : (kg + 1) * P].bitcast(FP8X4),
                        lhsT_scale=scales[:, m, kg * P : (kg + 1) * P],
                        rhs=words[:, kg, first : first + width].bitcast(FP8X4),
                        rhs_scale=planes[:, kg, column : column + width],
                        start=(count == 0),
                        stop=(count == last),
                    )
                    count += 1
            nc.vector.tensor_tensor(out=z, in0=acc[:, 0:width], in1=z, op=ADD)
            nc.scalar.activation(out=z, in_=z, func=FUNC.Tanh if gate == "g" else FUNC.Sigmoid)

        def product(gate, half, m, first, width):
            value = gate_values[gate, half][:, m, first : first + width]
            factor_column = m if gate == "f" else M_TILES + m
            if gate == "f":
                other = cx_sb[:, m, half * N_TILE + first : half * N_TILE + first + width]
            else:
                other = gate_values["g", half][:, m, first : first + width]
            nc.vector.scalar_tensor_tensor(
                out=value, in0=value, scalar=decay[:, factor_column : factor_column + 1], in1=other, op0=MULT, op1=MULT
            )

        def finish(gate, half, m, first, width):
            result = results.tile([P, N_TILE], F32, name="result")
            nc.vector.tensor_tensor(
                out=result[:, 0:width],
                in0=gate_values["i", half][:, m, first : first + width],
                in1=gate_values[gate, half][:, m, first : first + width],
                op=ADD,
            )
            column = half * N_TILE + first
            nc.sync.dma_start(out=out_by_tile[:, m, column : column + width], in_=result[:, 0:width])

        def bias_tiles(gate, half, who):
            return [m for m in range(M_TILES) if BIAS_ENGINE[gate, half][m] == who]

        spread = [block for block in BLOCKS if BIAS_ENGINE[block] != "tttt"]
        for m in range(M_TILES):
            transpose_tile("hx", hx_sb, m)
            if m % 2:
                quantise_pair("hx", m - 1)
            for block in spread[m:: M_TILES]:
                spread_bias(*block)
        spread_a_and_b()
        for m in range(M_TILES):
            transpose_tile("cx", cx_sb, m)
            if m % 2:
                quantise_pair("cx", m - 1)
        decay_factors()
        load_table(FUNC.Sigmoid)
        for block in BLOCKS:
            for m in bias_tiles(*block, "g"):
                add_bias(nc.gpsimd, *block, m)

        steps = [(gate, half, m, 0, N_TILE) for gate, half in BLOCKS for m in range(M_TILES)]
        gate, half, m, first, width = steps.pop()
        for piece in range(2):
            steps.append((gate, half, m, piece * N_TILE // 2, N_TILE // 2))
        for m in bias_tiles(*BLOCKS[0], "t"):
            add_bias_tensor(*BLOCKS[0], m)
        for s in range(len(steps) + 3):
            if s < len(steps):
                gate, half, m, first, width = steps[s]
                if m == 0:
                    for tile in bias_tiles(gate, half, "v"):
                        add_bias(nc.vector, gate, half, tile)
                multiply(*steps[s])
                if s + M_TILES < len(steps) and steps[s + M_TILES][3] == 0:
                    ahead = steps[s + M_TILES][:3]
                    if ahead[2] in bias_tiles(*ahead[:2], "t"):
                        add_bias_tensor(*ahead)
            if 2 <= s < len(steps) + 2 and steps[s - 2][0] != "g":
                product(*steps[s - 2])
            if s >= 3 and steps[s - 3][0] == "f":
                finish(*steps[s - 3])
